import numpy as np
import ml_dtypes


def mxq(x, axis, fmt="e4m3"):
    dtype, down = {"e4m3": (ml_dtypes.float8_e4m3fn, 7), "e5m2": (ml_dtypes.float8_e5m2, 14)}[fmt]
    v = np.moveaxis(np.asarray(x, np.float32).astype(ml_dtypes.bfloat16).astype(np.float64), axis, -1)
    blocks = v.reshape(v.shape[:-1] + (-1, 32))
    amax = np.abs(blocks).max(-1, keepdims=True)
    byte = np.maximum(np.where(amax > 0, np.frexp(amax)[1] - 1 + 127, 0) - down, 1)
    scale = np.exp2(byte - 127.0)
    codes = (blocks / scale).astype(np.float32).astype(dtype).astype(np.float64)
    return np.moveaxis((codes * scale).reshape(v.shape), -1, axis)


WIDE = False


def mx_kscale(k):
    if not WIDE:
        return np.ones(k)
    levels = np.array([10, -10, 5, -5, 0])
    if k % 512:
        return np.exp2(np.random.permutation(np.resize(levels, k // 32))).repeat(32)
    a = np.empty((k // 512, 16))
    for p in range(k // 512):
        a[p, :8] = np.random.permutation(np.resize(levels, 8))
        for g in range(8):
            far = levels[np.abs(levels - a[p, g]) >= 10]
            a[p, g + 8] = far[np.random.randint(len(far))]
    return np.exp2(a.ravel()).repeat(32)


BF16 = ml_dtypes.bfloat16


def bf(x):
    return np.asarray(x, np.float32).astype(BF16)


def f64(x):
    return np.asarray(x).astype(np.float64)


B, T, S, Dt, Df = 8, 512, 1024, 2048, 512
EPS = 1e-6


def rmsnorm(x, w):
    return x * (1.0 / np.sqrt(np.mean(x * x, axis=-1, keepdims=True) + EPS)) * w


def setup_inputs():
    s = mx_kscale(Df)
    return {"features": bf(np.random.standard_normal((B, S, Df))),
            "fn_w": bf((1.0 + 0.1 * np.random.standard_normal(Df)) * s),
            "Wk_w": bf(np.random.standard_normal((Df, Df)) / np.sqrt(Df) / s[None, :]),
            "Wk_b": bf(np.random.standard_normal(Df) * 0.3),
            "kn_w": bf(1.0 + 0.1 * np.random.standard_normal(Df))}


def reference(features, fn_w, Wk_w, Wk_b, kn_w):
    features_n = rmsnorm(f64(features), f64(fn_w))
    k = (mxq(features_n, 2, "e4m3") @ mxq(f64(Wk_w), 1, "e4m3").T) + f64(Wk_b)
    return rmsnorm(k, f64(kn_w))

@@ -1,0 +1,162 @@
+import concourse.mybir as mybir
+from concourse.masks import make_identity
+
+BF16 = mybir.dt.bfloat16
+F32 = mybir.dt.float32
+U32 = mybir.dt.uint32
+U8 = mybir.dt.uint8
+FP8X4 = mybir.dt.float8_e4m3fn_x4
+ACT = mybir.ActivationFunctionType
+ALU = mybir.AluOpType
+
+P = 128
+PACK = 4
+D = 512
+TOKENS = 8 * 1024
+SLOTS = 4
+GROUPS = TOKENS // (P * SLOTS)
+EPS = 1e-6
+
+FLOPS = 2 * TOKENS * D * D
+
+
+def tile_crossattention_pa_t_kernel(tc, features, fn_w, Wk_w, Wk_b, kn_w, out):
+    nc = tc.nc
+    x_dram = features.flatten_outer_dims().rearrange("(g p s) k -> g p s k", p=P, s=SLOTS)
+    out_dram = out.flatten_outer_dims().rearrange("(g p s) o -> g p s o", p=P, s=SLOTS)
+
+    with tc.tile_pool(name="const", bufs=1) as const, tc.tile_pool(name="resident", bufs=1) as resident, tc.tile_pool(
+        name="work", bufs=2
+    ) as work, tc.tile_pool(name="result", bufs=4) as result, tc.tile_pool(name="small", bufs=4) as small, tc.psum_pool(
+        name="turned_banks", bufs=4
+    ) as turned_banks, tc.psum_pool(name="product_banks", bufs=4) as product_banks:
+        eps = const.tile([P, 1], F32)
+        nc.vector.memset(eps[:], EPS)
+        warm = const.tile([P, 1], F32)
+        nc.scalar.activation(out=warm[:], in_=eps[:], func=ACT.Sqrt)
+        ident = const.tile([P, P], F32)
+        make_identity(nc, ident[:])
+
+        x_rows = []
+        w_rows = const.tile([P, SLOTS, D], BF16)
+        for g in range(GROUPS):
+            x_g = resident.tile([P, SLOTS, D], BF16, name="x%d" % g)
+            nc.sync.dma_start(out=x_g[:], in_=x_dram[g])
+            x_rows.append(x_g)
+            if g == 0:
+                nc.sync.dma_start(out=w_rows[:], in_=Wk_w.rearrange("(s p) k -> p s k", p=P))
+        fn_gain = const.tile([P, D], BF16)
+        nc.scalar.dma_start(out=fn_gain[:], in_=fn_w.partition_broadcast(P))
+        bias = const.tile([P, D], BF16)
+        nc.scalar.dma_start(out=bias[:], in_=Wk_b.partition_broadcast(P))
+        kn_gain = const.tile([P, D], BF16)
+        nc.scalar.dma_start(out=kn_gain[:], in_=kn_w.partition_broadcast(P))
+
+        def root_mean_square(rows):
+            sums = small.tile([P, SLOTS], F32)
+            for s in range(SLOTS):
+                squares = small.tile([P, D], BF16)
+                nc.scalar.activation(out=squares[:], in_=rows[:, s, :], func=ACT.Square, accum_out=sums[:, s : s + 1])
+            rms = small.tile([P, SLOTS], F32)
+            nc.scalar.activation(out=rms[:], in_=sums[:], func=ACT.Sqrt, scale=1.0 / D, bias=eps[:])
+            return rms
+
+        def invert(rms):
+            inverse = small.tile([P, SLOTS], F32)
+            nc.vector.reciprocal(out=inverse[:], in_=rms[:])
+            return inverse
+
+        def normalise(rows, inverse):
+            normed = work.tile([P, SLOTS, D], BF16)
+            for s in range(SLOTS):
+                nc.vector.scalar_tensor_tensor(
+                    out=normed[:, s, :],
+                    in0=rows[:, s, :],
+                    scalar=inverse[:, s : s + 1],
+                    in1=fn_gain[:],
+                    op0=ALU.mult,
+                    op1=ALU.mult,
+                )
+            return normed
+
+        def turn(rows):
+            grouped = work.tile([P, SLOTS, P, PACK], BF16, align_bytes=64)
+            for pair in range(SLOTS // 2):
+                turned = turned_banks.tile([P, 2, 2, P], F32)
+                for s in range(2):
+                    words = rows[:, 2 * pair + s, :].bitcast(F32)
+                    for u in range(2):
+                        nc.tensor.transpose(turned[:, s, u, :], words[:, u : D // 2 : 2], ident[:])
+                nc.scalar.copy(
+                    out=grouped[:, 2 * pair : 2 * pair + 2, :, :].rearrange("p s r t -> p (s r t)").bitcast(F32),
+                    in_=turned[:].rearrange("p s u r -> p s r u"),
+                )
+            return grouped
+
+        def quantise(grouped, codes, scales):
+            nc.vector.quantize_mx(
+                out=codes[:].bitcast(FP8X4), scales=scales[:], in_=grouped[:].rearrange("p s r t -> p (s r t)")
+            )
+
+        def multiply(codes, scales):
+            products = []
+            for s in range(SLOTS):
+                product = product_banks.tile([P, D], F32)
+                nc.tensor.matmul_mx(
+                    out=product[:],
+                    lhsT=codes[:, s * P : (s + 1) * P].bitcast(FP8X4),
+                    lhsT_scale=scales[:, s * P : (s + 1) * P],
+                    rhs=w_codes[:].bitcast(FP8X4),
+                    rhs_scale=w_scales[:],
+                    start=True,
+                    stop=True,
+                )
+                products.append(product)
+            return products
+
+        def add_bias(products):
+            biased = result.tile([P, SLOTS, D], F32)
+            for s in range(SLOTS):
+                nc.vector.tensor_tensor(out=biased[:, s, :], in0=products[s][:], in1=bias[:], op=ALU.add)
+            return biased
+
+        def finish(g, biased, inverse):
+            for s in range(SLOTS):
+                nc.vector.scalar_tensor_tensor(
+                    out=biased[:, s, :],
+                    in0=biased[:, s, :],
+                    scalar=inverse[:, s : s + 1],
+                    in1=kn_gain[:],
+                    op0=ALU.mult,
+                    op1=ALU.mult,
+                )
+            nc.sync.dma_start(out=out_dram[g], in_=biased[:])
+
+        w_codes = const.tile([P, D], U32, align_bytes=64)
+        w_scales = const.tile([P, D], U8, align_bytes=64)
+        quantise(turn(w_rows), w_codes, w_scales)
+
+        x_inverse = {0: invert(root_mean_square(x_rows[0]))}
+        products, biased, k_inverse = {}, {}, {}
+        for i in range(GROUPS + 2):
+            if i < GROUPS:
+                normed = normalise(x_rows[i], x_inverse[i])
+            if i + 1 < GROUPS:
+                x_rms = root_mean_square(x_rows[i + 1])
+            if i < GROUPS:
+                grouped = turn(normed)
+            if 0 <= i - 1 < GROUPS:
+                biased[i - 1] = add_bias(products[i - 1])
+            if i + 1 < GROUPS:
+                x_inverse[i + 1] = invert(x_rms)
+            if i < GROUPS:
+                codes = work.tile([P, SLOTS * P], U32, align_bytes=64)
+                scales = work.tile([P, SLOTS * P], U8, align_bytes=64)
+                quantise(grouped, codes, scales)
+                products[i] = multiply(codes, scales)
+            if 0 <= i - 1 < GROUPS:
+                k_rms = root_mean_square(biased[i - 1])
+            if 0 <= i - 2:
+                finish(i - 2, biased[i - 2], k_inverse[i - 2])
+            if 0 <= i - 1 < GROUPS:
+                k_inverse[i - 1] = invert(k_rms)

@@ -14,8 +14,11 @@ PACK = 4
 D = 512
 TOKENS = 8 * 1024
 SLOTS = 4
+PAIRS = SLOTS // 2
 GROUPS = TOKENS // (P * SLOTS)
 EPS = 1e-6
+GPSIMD_SLOTS = 2
+HEAD_GROUPS = 2
 
 FLOPS = 2 * TOKENS * D * D
 
@@ -27,136 +30,222 @@ def tile_crossattention_pa_t_kernel(tc, features, fn_w, Wk_w, Wk_b, kn_w, out):
 
     with tc.tile_pool(name="const", bufs=1) as const, tc.tile_pool(name="resident", bufs=1) as resident, tc.tile_pool(
         name="work", bufs=2
-    ) as work, tc.tile_pool(name="result", bufs=4) as result, tc.tile_pool(name="small", bufs=4) as small, tc.psum_pool(
-        name="turned_banks", bufs=4
-    ) as turned_banks, tc.psum_pool(name="product_banks", bufs=4) as product_banks:
+    ) as work, tc.tile_pool(name="result", bufs=6) as result, tc.tile_pool(name="small", bufs=4) as small, tc.psum_pool(
+        name="turned_banks", bufs=3
+    ) as turned_banks, tc.psum_pool(name="product_banks", bufs=4) as product_banks, tc.psum_pool(
+        name="gain_bank", bufs=1
+    ) as gain_bank, tc.manual_schedule():
         eps = const.tile([P, 1], F32)
         nc.vector.memset(eps[:], EPS)
         warm = const.tile([P, 1], F32)
         nc.scalar.activation(out=warm[:], in_=eps[:], func=ACT.Sqrt)
         ident = const.tile([P, P], F32)
         make_identity(nc, ident[:])
+        fn_row = const.tile([P, D], BF16)
+        nc.vector.memset(fn_row[:], 0.0)
+        other_rows = const.tile([P, 2, D], BF16)
+        nc.gpsimd.memset(other_rows[:], 0.0)
+        ones_row = const.tile([P, P], BF16)
+        nc.vector.memset(ones_row[:], 0.0)
+        nc.vector.memset(ones_row[0:1, :], 1.0)
+
+        def load_row(row, source):
+            nc.sync.dma_start(out=row, in_=source.rearrange("(a d) -> a d", a=1))
 
         x_rows = []
         w_rows = const.tile([P, SLOTS, D], BF16)
         for g in range(GROUPS):
             x_g = resident.tile([P, SLOTS, D], BF16, name="x%d" % g)
-            nc.sync.dma_start(out=x_g[:], in_=x_dram[g])
             x_rows.append(x_g)
             if g == 0:
+                for s in range(SLOTS):
+                    nc.sync.dma_start(out=x_g[:, s, :], in_=x_dram[g, :, s, :])
+                    if s == 0:
+                        load_row(fn_row[0:1, :], fn_w)
+                load_row(other_rows[0:1, 0, :], kn_w)
+                load_row(other_rows[0:1, 1, :], Wk_b)
                 nc.sync.dma_start(out=w_rows[:], in_=Wk_w.rearrange("(s p) k -> p s k", p=P))
-        fn_gain = const.tile([P, D], BF16)
-        nc.scalar.dma_start(out=fn_gain[:], in_=fn_w.partition_broadcast(P))
-        bias = const.tile([P, D], BF16)
-        nc.scalar.dma_start(out=bias[:], in_=Wk_b.partition_broadcast(P))
-        kn_gain = const.tile([P, D], BF16)
-        nc.scalar.dma_start(out=kn_gain[:], in_=kn_w.partition_broadcast(P))
+            else:
+                nc.sync.dma_start(out=x_g[:], in_=x_dram[g])
 
-        def root_mean_square(rows):
-            sums = small.tile([P, SLOTS], F32)
-            for s in range(SLOTS):
-                squares = small.tile([P, D], BF16)
-                nc.scalar.activation(out=squares[:], in_=rows[:, s, :], func=ACT.Square, accum_out=sums[:, s : s + 1])
-            rms = small.tile([P, SLOTS], F32)
-            nc.scalar.activation(out=rms[:], in_=sums[:], func=ACT.Sqrt, scale=1.0 / D, bias=eps[:])
+        def scalar_square_sum(row, total):
+            squares = small.tile([P, D], BF16)
+            nc.scalar.activation(out=squares[:], in_=row, func=ACT.Square, accum_out=total)
+
+        def vector_square_sum(row, total):
+            products = small.tile([P, D], BF16)
+            nc.vector.scalar_tensor_tensor(
+                out=products[:], in0=row, scalar=1.0, in1=row, op0=ALU.mult, op1=ALU.mult, accum_out=total
+            )
+
+        def first_square_sum(g, s, totals):
+            if g < HEAD_GROUPS and s >= SLOTS // 2:
+                vector_square_sum(x_rows[g][:, s, :], totals[:, s : s + 1])
+            else:
+                scalar_square_sum(x_rows[g][:, s, :], totals[:, s : s + 1])
+
+        def root(totals, first, last):
+            rms = small.tile([P, 2 * SLOTS], F32)
+            nc.scalar.activation(
+                out=rms[:, first:last], in_=totals[:, first:last], func=ACT.Sqrt, scale=1.0 / D, bias=eps[:]
+            )
             return rms
 
-        def invert(rms):
-            inverse = small.tile([P, SLOTS], F32)
-            nc.vector.reciprocal(out=inverse[:], in_=rms[:])
+        def invert(rms, first, last):
+            inverse = small.tile([P, 2 * SLOTS], F32)
+            nc.vector.reciprocal(out=inverse[:, first:last], in_=rms[:, first:last])
             return inverse
 
-        def normalise(rows, inverse):
-            normed = work.tile([P, SLOTS, D], BF16)
-            for s in range(SLOTS):
-                nc.vector.scalar_tensor_tensor(
-                    out=normed[:, s, :],
-                    in0=rows[:, s, :],
-                    scalar=inverse[:, s : s + 1],
-                    in1=fn_gain[:],
-                    op0=ALU.mult,
-                    op1=ALU.mult,
-                )
-            return normed
+        def normalise(g, s, inverse, normed):
+            nc.vector.scalar_tensor_tensor(
+                out=normed[:, s, :],
+                in0=x_rows[g][:, s, :],
+                scalar=inverse[:, s : s + 1],
+                in1=gains[:, 0, :],
+                op0=ALU.mult,
+                op1=ALU.mult,
+            )
 
-        def turn(rows):
-            grouped = work.tile([P, SLOTS, P, PACK], BF16, align_bytes=64)
-            for pair in range(SLOTS // 2):
-                turned = turned_banks.tile([P, 2, 2, P], F32)
-                for s in range(2):
-                    words = rows[:, 2 * pair + s, :].bitcast(F32)
-                    for u in range(2):
-                        nc.tensor.transpose(turned[:, s, u, :], words[:, u : D // 2 : 2], ident[:])
-                nc.scalar.copy(
-                    out=grouped[:, 2 * pair : 2 * pair + 2, :, :].rearrange("p s r t -> p (s r t)").bitcast(F32),
-                    in_=turned[:].rearrange("p s u r -> p s r u"),
-                )
-            return grouped
+        def turn(rows, pair):
+            turned = turned_banks.tile([P, 2, 2, P], F32)
+            for s in range(2):
+                words = rows[:, 2 * pair + s, :].bitcast(F32)
+                for u in range(2):
+                    nc.tensor.transpose(turned[:, s, u, :], words[:, u : D // 2 : 2], ident[:])
+            return turned
+
+        def regroup(turned, pair, grouped):
+            nc.scalar.copy(
+                out=grouped[:, 2 * pair : 2 * pair + 2, :, :].rearrange("p s r t -> p (s r t)").bitcast(F32),
+                in_=turned[:].rearrange("p s u r -> p s r u"),
+            )
 
         def quantise(grouped, codes, scales):
             nc.vector.quantize_mx(
                 out=codes[:].bitcast(FP8X4), scales=scales[:], in_=grouped[:].rearrange("p s r t -> p (s r t)")
             )
 
-        def multiply(codes, scales):
-            products = []
-            for s in range(SLOTS):
-                product = product_banks.tile([P, D], F32)
-                nc.tensor.matmul_mx(
-                    out=product[:],
-                    lhsT=codes[:, s * P : (s + 1) * P].bitcast(FP8X4),
-                    lhsT_scale=scales[:, s * P : (s + 1) * P],
-                    rhs=w_codes[:].bitcast(FP8X4),
-                    rhs_scale=w_scales[:],
-                    start=True,
-                    stop=True,
-                )
-                products.append(product)
-            return products
+        def multiply(codes, scales, s):
+            product = product_banks.tile([P, D], F32)
+            nc.tensor.matmul_mx(
+                out=product[:],
+                lhsT=codes[:, s * P : (s + 1) * P].bitcast(FP8X4),
+                lhsT_scale=scales[:, s * P : (s + 1) * P],
+                rhs=w_codes[:].bitcast(FP8X4),
+                rhs_scale=w_scales[:],
+                start=True,
+                stop=True,
+            )
+            return product
 
-        def add_bias(products):
-            biased = result.tile([P, SLOTS, D], F32)
-            for s in range(SLOTS):
-                nc.vector.tensor_tensor(out=biased[:, s, :], in0=products[s][:], in1=bias[:], op=ALU.add)
-            return biased
+        def add_bias(product, biased, s):
+            nc.vector.tensor_tensor(out=biased[:, s, :], in0=product[:], in1=bias[:], op=ALU.add)
 
-        def finish(g, biased, inverse):
+        def vector_finish(biased, s, inverse):
+            nc.vector.scalar_tensor_tensor(
+                out=biased[:, s, :],
+                in0=biased[:, s, :],
+                scalar=inverse,
+                in1=gains[:, 1, :],
+                op0=ALU.mult,
+                op1=ALU.mult,
+            )
+
+        def gpsimd_finish(biased, s, inverse):
+            nc.gpsimd.tensor_scalar(
+                out=biased[:, s, :], in0=biased[:, s, :], scalar1=inverse, scalar2=0.0, op0=ALU.mult, op1=ALU.add
+            )
+            nc.gpsimd.tensor_tensor(out=biased[:, s, :], in0=biased[:, s, :], in1=kn_gain_sbuf[:], op=ALU.mult)
+
+        def finish(g, biased, inverse, gpsimd_slots):
             for s in range(SLOTS):
-                nc.vector.scalar_tensor_tensor(
-                    out=biased[:, s, :],
-                    in0=biased[:, s, :],
-                    scalar=inverse[:, s : s + 1],
-                    in1=kn_gain[:],
-                    op0=ALU.mult,
-                    op1=ALU.mult,
-                )
+                column = inverse[:, SLOTS + s : SLOTS + s + 1]
+                if s < gpsimd_slots:
+                    gpsimd_finish(biased, s, column)
+                else:
+                    vector_finish(biased, s, column)
             nc.sync.dma_start(out=out_dram[g], in_=biased[:])
+
+        totals = small.tile([P, 2 * SLOTS], F32, name="totals")
+        for s in range(SLOTS):
+            first_square_sum(0, s, totals)
+        inverse = invert(root(totals, 0, SLOTS), 0, SLOTS)
+
+        gains = gain_bank.tile([P, 2, D], BF16)
+        nc.tensor.matmul(gains[:, 0, :], lhsT=ones_row[:], rhs=fn_row[:], start=True, stop=True)
+        normed = work.tile([P, SLOTS, D], BF16, name="normed")
+        for s in range(SLOTS):
+            normalise(0, s, inverse, normed)
 
         w_codes = const.tile([P, D], U32, align_bytes=64)
         w_scales = const.tile([P, D], U8, align_bytes=64)
-        quantise(turn(w_rows), w_codes, w_scales)
+        w_grouped = const.tile([P, SLOTS, P, PACK], BF16, align_bytes=64)
+        for pair in range(PAIRS):
+            regroup(turn(w_rows, pair), pair, w_grouped)
 
-        x_inverse = {0: invert(root_mean_square(x_rows[0]))}
-        products, biased, k_inverse = {}, {}, {}
-        for i in range(GROUPS + 2):
-            if i < GROUPS:
-                normed = normalise(x_rows[i], x_inverse[i])
+        totals = small.tile([P, 2 * SLOTS], F32, name="totals")
+        for s in range(SLOTS):
+            first_square_sum(1, s, totals)
+        quantise(w_grouped, w_codes, w_scales)
+
+        grouped = work.tile([P, SLOTS, P, PACK], BF16, align_bytes=64, name="grouped")
+        turned = [turn(normed, pair) for pair in range(PAIRS)]
+        bias = const.tile([P, D], F32)
+        kn_gain_sbuf = const.tile([P, D], F32)
+        nc.tensor.matmul(gains[:, 1, :], lhsT=ones_row[:], rhs=other_rows[:, 0, :], start=True, stop=True)
+        regroup(turned[0], 0, grouped)
+        rms = root(totals, 0, SLOTS)
+
+        products, biased = {}, {}
+        for i in range(GROUPS):
+            totals = small.tile([P, 2 * SLOTS], F32, name="totals")
+            regroup(turned[1], 1, grouped)
+            if i == 0:
+                for copy, v in ((bias, 1), (kn_gain_sbuf, 0)):
+                    spread = turned_banks.tile([P, D], F32, name="turned")
+                    nc.tensor.matmul(spread[:], lhsT=ones_row[:], rhs=other_rows[:, v, :], start=True, stop=True)
+                    nc.scalar.copy(out=copy[:], in_=spread[:])
+            codes = work.tile([P, SLOTS * P], U32, align_bytes=64)
+            scales = work.tile([P, SLOTS * P], U8, align_bytes=64)
+            if i >= 1:
+                biased[i - 1] = result.tile([P, SLOTS, D], F32, name="biased")
+            for s in range(SLOTS):
+                if i + 2 < GROUPS:
+                    first_square_sum(i + 2, s, totals)
+                if i >= 1:
+                    add_bias(products[s], biased[i - 1], s)
+                    scalar_square_sum(biased[i - 1][:, s, :], totals[:, SLOTS + s : SLOTS + s + 1])
+                if s == 1:
+                    quantise(grouped, codes, scales)
+                if s == 2:
+                    inverse = invert(rms, 0 if i + 1 < GROUPS else SLOTS, 2 * SLOTS if i >= 2 else SLOTS)
+            if i >= 2:
+                finish(i - 2, biased[i - 2], inverse, GPSIMD_SLOTS)
+            for s in range(SLOTS):
+                products[s] = multiply(codes, scales, s)
+            if i + 2 < GROUPS or i >= 1:
+                rms = root(totals, 0 if i + 2 < GROUPS else SLOTS, 2 * SLOTS if i >= 1 else SLOTS)
             if i + 1 < GROUPS:
-                x_rms = root_mean_square(x_rows[i + 1])
-            if i < GROUPS:
-                grouped = turn(normed)
-            if 0 <= i - 1 < GROUPS:
-                biased[i - 1] = add_bias(products[i - 1])
-            if i + 1 < GROUPS:
-                x_inverse[i + 1] = invert(x_rms)
-            if i < GROUPS:
-                codes = work.tile([P, SLOTS * P], U32, align_bytes=64)
-                scales = work.tile([P, SLOTS * P], U8, align_bytes=64)
-                quantise(grouped, codes, scales)
-                products[i] = multiply(codes, scales)
-            if 0 <= i - 1 < GROUPS:
-                k_rms = root_mean_square(biased[i - 1])
-            if 0 <= i - 2:
-                finish(i - 2, biased[i - 2], k_inverse[i - 2])
-            if 0 <= i - 1 < GROUPS:
-                k_inverse[i - 1] = invert(k_rms)
+                normed = work.tile([P, SLOTS, D], BF16, name="normed")
+                grouped = work.tile([P, SLOTS, P, PACK], BF16, align_bytes=64, name="grouped")
+                turned = []
+                for pair in range(PAIRS):
+                    for s in (2 * pair, 2 * pair + 1):
+                        normalise(i + 1, s, inverse, normed)
+                    turned.append(turn(normed, pair))
+                regroup(turned[0], 0, grouped)
+
+        last = result.tile([P, SLOTS, D], F32, name="biased")
+        totals = small.tile([P, 2 * SLOTS], F32, name="totals")
+        roots = []
+        for pair in range(PAIRS):
+            for s in (2 * pair, 2 * pair + 1):
+                add_bias(products[s], last, s)
+                scalar_square_sum(last[:, s, :], totals[:, s : s + 1])
+            roots.append(root(totals, 2 * pair, 2 * pair + 2))
+        finish(GROUPS - 2, biased[GROUPS - 2], invert(rms, SLOTS, 2 * SLOTS), 1)
+        for pair in range(PAIRS):
+            inverse = invert(roots[pair], 2 * pair, 2 * pair + 2)
+            for s in (2 * pair, 2 * pair + 1):
+                vector_finish(last, s, inverse[:, s : s + 1])
+                nc.sync.dma_start(out=out_dram[GROUPS - 1, :, s, :], in_=last[:, s, :])

@@ -17,7 +17,7 @@ SLOTS = 4
 PAIRS = SLOTS // 2
 GROUPS = TOKENS // (P * SLOTS)
 EPS = 1e-6
-GPSIMD_SLOTS = 2
+GPSIMD_SLOTS = 3
 HEAD_GROUPS = 2
 
 FLOPS = 2 * TOKENS * D * D
@@ -157,7 +157,8 @@ def tile_crossattention_pa_t_kernel(tc, features, fn_w, Wk_w, Wk_b, kn_w, out):
             )
             nc.gpsimd.tensor_tensor(out=biased[:, s, :], in0=biased[:, s, :], in1=kn_gain_sbuf[:], op=ALU.mult)
 
-        def finish(g, biased, inverse, gpsimd_slots):
+        def finish(g, biased, inverse):
+            gpsimd_slots = min(GPSIMD_SLOTS, GROUPS - 1 - g)
             for s in range(SLOTS):
                 column = inverse[:, SLOTS + s : SLOTS + s + 1]
                 if s < gpsimd_slots:
@@ -217,10 +218,9 @@ def tile_crossattention_pa_t_kernel(tc, features, fn_w, Wk_w, Wk_b, kn_w, out):
                     scalar_square_sum(biased[i - 1][:, s, :], totals[:, SLOTS + s : SLOTS + s + 1])
                 if s == 1:
                     quantise(grouped, codes, scales)
-                if s == 2:
                     inverse = invert(rms, 0 if i + 1 < GROUPS else SLOTS, 2 * SLOTS if i >= 2 else SLOTS)
             if i >= 2:
-                finish(i - 2, biased[i - 2], inverse, GPSIMD_SLOTS)
+                finish(i - 2, biased[i - 2], inverse)
             for s in range(SLOTS):
                 products[s] = multiply(codes, scales, s)
             if i + 2 < GROUPS or i >= 1:
@@ -243,7 +243,7 @@ def tile_crossattention_pa_t_kernel(tc, features, fn_w, Wk_w, Wk_b, kn_w, out):
                 add_bias(products[s], last, s)
                 scalar_square_sum(last[:, s, :], totals[:, s : s + 1])
             roots.append(root(totals, 2 * pair, 2 * pair + 2))
-        finish(GROUPS - 2, biased[GROUPS - 2], invert(rms, SLOTS, 2 * SLOTS), 1)
+        finish(GROUPS - 2, biased[GROUPS - 2], invert(rms, SLOTS, 2 * SLOTS))
         for pair in range(PAIRS):
             inverse = invert(roots[pair], 2 * pair, 2 * pair + 2)
             for s in (2 * pair, 2 * pair + 1):

@@ -17,8 +17,7 @@ SLOTS = 4
 PAIRS = SLOTS // 2
 GROUPS = TOKENS // (P * SLOTS)
 EPS = 1e-6
-GPSIMD_SLOTS = 3
-HEAD_GROUPS = 2
+GPSIMD_SLOTS = (3, 2)
 
 FLOPS = 2 * TOKENS * D * D
 
@@ -62,11 +61,12 @@ def tile_crossattention_pa_t_kernel(tc, features, fn_w, Wk_w, Wk_b, kn_w, out):
                     nc.sync.dma_start(out=x_g[:, s, :], in_=x_dram[g, :, s, :])
                     if s == 0:
                         load_row(fn_row[0:1, :], fn_w)
-                load_row(other_rows[0:1, 0, :], kn_w)
-                load_row(other_rows[0:1, 1, :], Wk_b)
-                nc.sync.dma_start(out=w_rows[:], in_=Wk_w.rearrange("(s p) k -> p s k", p=P))
             else:
                 nc.sync.dma_start(out=x_g[:], in_=x_dram[g])
+            if g == 1:
+                nc.sync.dma_start(out=w_rows[:], in_=Wk_w.rearrange("(s p) k -> p s k", p=P))
+                load_row(other_rows[0:1, 0, :], kn_w)
+                load_row(other_rows[0:1, 1, :], Wk_b)
 
         def scalar_square_sum(row, total):
             squares = small.tile([P, D], BF16)
@@ -77,12 +77,6 @@ def tile_crossattention_pa_t_kernel(tc, features, fn_w, Wk_w, Wk_b, kn_w, out):
             nc.vector.scalar_tensor_tensor(
                 out=products[:], in0=row, scalar=1.0, in1=row, op0=ALU.mult, op1=ALU.mult, accum_out=total
             )
-
-        def first_square_sum(g, s, totals):
-            if g < HEAD_GROUPS and s >= SLOTS // 2:
-                vector_square_sum(x_rows[g][:, s, :], totals[:, s : s + 1])
-            else:
-                scalar_square_sum(x_rows[g][:, s, :], totals[:, s : s + 1])
 
         def root(totals, first, last):
             rms = small.tile([P, 2 * SLOTS], F32)
@@ -151,88 +145,120 @@ def tile_crossattention_pa_t_kernel(tc, features, fn_w, Wk_w, Wk_b, kn_w, out):
                 op1=ALU.mult,
             )
 
-        def gpsimd_finish(biased, s, inverse):
-            nc.gpsimd.tensor_scalar(
-                out=biased[:, s, :], in0=biased[:, s, :], scalar1=inverse, scalar2=0.0, op0=ALU.mult, op1=ALU.add
-            )
-            nc.gpsimd.tensor_tensor(out=biased[:, s, :], in0=biased[:, s, :], in1=kn_gain_sbuf[:], op=ALU.mult)
-
         def finish(g, biased, inverse):
-            gpsimd_slots = min(GPSIMD_SLOTS, GROUPS - 1 - g)
-            for s in range(SLOTS):
-                column = inverse[:, SLOTS + s : SLOTS + s + 1]
-                if s < gpsimd_slots:
-                    gpsimd_finish(biased, s, column)
-                else:
-                    vector_finish(biased, s, column)
-            nc.sync.dma_start(out=out_dram[g], in_=biased[:])
+            shared = min(GPSIMD_SLOTS[g % 2], GROUPS - 1 - g)
+            for s in range(shared):
+                nc.gpsimd.tensor_scalar(
+                    out=biased[:, s, :],
+                    in0=biased[:, s, :],
+                    scalar1=inverse[:, SLOTS + s : SLOTS + s + 1],
+                    scalar2=0.0,
+                    op0=ALU.mult,
+                    op1=ALU.add,
+                )
+            nc.gpsimd.tensor_tensor(
+                out=biased[:, :shared, :],
+                in0=biased[:, :shared, :],
+                in1=kn_gain_sbuf[:].unsqueeze(1).to_broadcast([P, shared, D]),
+                op=ALU.mult,
+            )
+            for s in range(shared, SLOTS):
+                vector_finish(biased, s, inverse[:, SLOTS + s : SLOTS + s + 1])
+            queue = nc.scalar if g == GROUPS - 2 else nc.sync
+            queue.dma_start(out=out_dram[g], in_=biased[:])
 
-        totals = small.tile([P, 2 * SLOTS], F32, name="totals")
-        for s in range(SLOTS):
-            first_square_sum(0, s, totals)
-        inverse = invert(root(totals, 0, SLOTS), 0, SLOTS)
+        def spread_vector(v):
+            copy = const.tile([P, D], F32, name="vector%d" % v)
+            bank = turned_banks.tile([P, D], F32, name="turned")
+            nc.tensor.matmul(bank[:], lhsT=ones_row[:], rhs=other_rows[:, v, :], start=True, stop=True)
+            nc.scalar.copy(out=copy[:], in_=bank[:])
+            return copy
 
         gains = gain_bank.tile([P, 2, D], BF16)
         nc.tensor.matmul(gains[:, 0, :], lhsT=ones_row[:], rhs=fn_row[:], start=True, stop=True)
+        totals = small.tile([P, 2 * SLOTS], F32, name="totals")
         normed = work.tile([P, SLOTS, D], BF16, name="normed")
-        for s in range(SLOTS):
+        turned = {}
+        scalar_square_sum(x_rows[0][:, 0, :], totals[:, 0:1])
+        vector_square_sum(x_rows[0][:, 1, :], totals[:, 1:2])
+        inverse = invert(root(totals, 0, 2), 0, 2)
+        for s in (2, 3):
+            scalar_square_sum(x_rows[0][:, s, :], totals[:, s : s + 1])
+        rms = root(totals, 2, SLOTS)
+        for s in (0, 1):
             normalise(0, s, inverse, normed)
+        turned[0] = turn(normed, 0)
+        inverse = invert(rms, 2, SLOTS)
+        for s in (2, 3):
+            normalise(0, s, inverse, normed)
+        turned[1] = turn(normed, 1)
 
+        totals = small.tile([P, 2 * SLOTS], F32, name="totals")
+        for s in range(SLOTS):
+            scalar_square_sum(x_rows[1][:, s, :], totals[:, s : s + 1])
+        rms = root(totals, 0, SLOTS)
+        grouped = work.tile([P, SLOTS, P, PACK], BF16, align_bytes=64, name="grouped")
+        for pair in range(PAIRS):
+            regroup(turned[pair], pair, grouped)
         w_codes = const.tile([P, D], U32, align_bytes=64)
         w_scales = const.tile([P, D], U8, align_bytes=64)
         w_grouped = const.tile([P, SLOTS, P, PACK], BF16, align_bytes=64)
         for pair in range(PAIRS):
             regroup(turn(w_rows, pair), pair, w_grouped)
 
-        totals = small.tile([P, 2 * SLOTS], F32, name="totals")
-        for s in range(SLOTS):
-            first_square_sum(1, s, totals)
-        quantise(w_grouped, w_codes, w_scales)
-
-        grouped = work.tile([P, SLOTS, P, PACK], BF16, align_bytes=64, name="grouped")
-        turned = [turn(normed, pair) for pair in range(PAIRS)]
-        bias = const.tile([P, D], F32)
-        kn_gain_sbuf = const.tile([P, D], F32)
+        inverse = invert(rms, 0, SLOTS)
+        normed = work.tile([P, SLOTS, D], BF16, name="normed")
+        for pair in range(PAIRS):
+            for s in (2 * pair, 2 * pair + 1):
+                normalise(1, s, inverse, normed)
+            turned[pair] = turn(normed, pair)
         nc.tensor.matmul(gains[:, 1, :], lhsT=ones_row[:], rhs=other_rows[:, 0, :], start=True, stop=True)
-        regroup(turned[0], 0, grouped)
-        rms = root(totals, 0, SLOTS)
+        quantise(w_grouped, w_codes, w_scales)
+        bias = spread_vector(1)
 
         products, biased = {}, {}
         for i in range(GROUPS):
             totals = small.tile([P, 2 * SLOTS], F32, name="totals")
-            regroup(turned[1], 1, grouped)
             if i == 0:
-                for copy, v in ((bias, 1), (kn_gain_sbuf, 0)):
-                    spread = turned_banks.tile([P, D], F32, name="turned")
-                    nc.tensor.matmul(spread[:], lhsT=ones_row[:], rhs=other_rows[:, v, :], start=True, stop=True)
-                    nc.scalar.copy(out=copy[:], in_=spread[:])
+                next_grouped = work.tile([P, SLOTS, P, PACK], BF16, align_bytes=64, name="grouped")
+                for pair in range(PAIRS):
+                    regroup(turned[pair], pair, next_grouped)
             codes = work.tile([P, SLOTS * P], U32, align_bytes=64)
             scales = work.tile([P, SLOTS * P], U8, align_bytes=64)
             if i >= 1:
                 biased[i - 1] = result.tile([P, SLOTS, D], F32, name="biased")
             for s in range(SLOTS):
-                if i + 2 < GROUPS:
-                    first_square_sum(i + 2, s, totals)
+                if i + 2 < GROUPS and not (i == 0 and s >= 2):
+                    scalar_square_sum(x_rows[i + 2][:, s, :], totals[:, s : s + 1])
+                if i >= 2 and s == 0:
+                    regroup(turned[1], 1, grouped)
                 if i >= 1:
                     add_bias(products[s], biased[i - 1], s)
                     scalar_square_sum(biased[i - 1][:, s, :], totals[:, SLOTS + s : SLOTS + s + 1])
-                if s == 1:
+                if s == (2 if i + 1 < GROUPS else 1):
                     quantise(grouped, codes, scales)
-                    inverse = invert(rms, 0 if i + 1 < GROUPS else SLOTS, 2 * SLOTS if i >= 2 else SLOTS)
+                    if i >= 1:
+                        inverse = invert(rms, 0 if i + 1 < GROUPS else SLOTS, 2 * SLOTS if i >= 2 else SLOTS)
+            if i == 0:
+                for s in (2, 3):
+                    vector_square_sum(x_rows[2][:, s, :], totals[:, s : s + 1])
             if i >= 2:
                 finish(i - 2, biased[i - 2], inverse)
             for s in range(SLOTS):
                 products[s] = multiply(codes, scales, s)
             if i + 2 < GROUPS or i >= 1:
                 rms = root(totals, 0 if i + 2 < GROUPS else SLOTS, 2 * SLOTS if i >= 1 else SLOTS)
-            if i + 1 < GROUPS:
+            if i == 1:
+                kn_gain_sbuf = spread_vector(0)
+            if i == 0:
+                grouped = next_grouped
+            elif i + 1 < GROUPS:
                 normed = work.tile([P, SLOTS, D], BF16, name="normed")
-                grouped = work.tile([P, SLOTS, P, PACK], BF16, align_bytes=64, name="grouped")
-                turned = []
                 for pair in range(PAIRS):
                     for s in (2 * pair, 2 * pair + 1):
                         normalise(i + 1, s, inverse, normed)
-                    turned.append(turn(normed, pair))
+                    turned[pair] = turn(normed, pair)
+                grouped = work.tile([P, SLOTS, P, PACK], BF16, align_bytes=64, name="grouped")
                 regroup(turned[0], 0, grouped)
 
         last = result.tile([P, SLOTS, D], F32, name="biased")

@@ -17,7 +17,7 @@ SLOTS = 4
 PAIRS = SLOTS // 2
 GROUPS = TOKENS // (P * SLOTS)
 EPS = 1e-6
-GPSIMD_SLOTS = (3, 2)
+GPSIMD_COLUMNS = 2 * D + D // 2
 
 FLOPS = 2 * TOKENS * D * D
 
@@ -135,44 +135,41 @@ def tile_crossattention_pa_t_kernel(tc, features, fn_w, Wk_w, Wk_b, kn_w, out):
         def add_bias(product, biased, s):
             nc.vector.tensor_tensor(out=biased[:, s, :], in0=product[:], in1=bias[:], op=ALU.add)
 
-        def vector_finish(biased, s, inverse):
+        def vector_finish(biased, s, first, inverse):
             nc.vector.scalar_tensor_tensor(
-                out=biased[:, s, :],
-                in0=biased[:, s, :],
+                out=biased[:, s, first:],
+                in0=biased[:, s, first:],
                 scalar=inverse,
-                in1=gains[:, 1, :],
+                in1=gains[:, 1, first:],
                 op0=ALU.mult,
                 op1=ALU.mult,
             )
 
         def finish(g, biased, inverse):
-            shared = min(GPSIMD_SLOTS[g % 2], GROUPS - 1 - g)
-            for s in range(shared):
-                nc.gpsimd.tensor_scalar(
-                    out=biased[:, s, :],
-                    in0=biased[:, s, :],
-                    scalar1=inverse[:, SLOTS + s : SLOTS + s + 1],
-                    scalar2=0.0,
-                    op0=ALU.mult,
-                    op1=ALU.add,
-                )
-            nc.gpsimd.tensor_tensor(
-                out=biased[:, :shared, :],
-                in0=biased[:, :shared, :],
-                in1=kn_gain_sbuf[:].unsqueeze(1).to_broadcast([P, shared, D]),
-                op=ALU.mult,
-            )
-            for s in range(shared, SLOTS):
-                vector_finish(biased, s, inverse[:, SLOTS + s : SLOTS + s + 1])
+            shared = min(GPSIMD_COLUMNS, (GROUPS - 1 - g) * D)
+            for s in range(SLOTS):
+                ours = min(max(shared - s * D, 0), D)
+                if ours > 0:
+                    nc.gpsimd.tensor_scalar(
+                        out=biased[:, s, :ours],
+                        in0=biased[:, s, :ours],
+                        scalar1=inverse[:, SLOTS + s : SLOTS + s + 1],
+                        scalar2=0.0,
+                        op0=ALU.mult,
+                        op1=ALU.add,
+                    )
+                if ours < D:
+                    vector_finish(biased, s, ours, inverse[:, SLOTS + s : SLOTS + s + 1])
+            flat = biased[:].rearrange("p s o -> p (s o)")[:, :shared]
+            kn_flat = kn_gain_sbuf[:].rearrange("p s o -> p (s o)")[:, :shared]
+            nc.gpsimd.tensor_tensor(out=flat, in0=flat, in1=kn_flat, op=ALU.mult)
             queue = nc.scalar if g == GROUPS - 2 else nc.sync
             queue.dma_start(out=out_dram[g], in_=biased[:])
 
-        def spread_vector(v):
-            copy = const.tile([P, D], F32, name="vector%d" % v)
+        def spread_vector(v, copy):
             bank = turned_banks.tile([P, D], F32, name="turned")
             nc.tensor.matmul(bank[:], lhsT=ones_row[:], rhs=other_rows[:, v, :], start=True, stop=True)
-            nc.scalar.copy(out=copy[:], in_=bank[:])
-            return copy
+            nc.scalar.copy(out=copy, in_=bank[:])
 
         gains = gain_bank.tile([P, 2, D], BF16)
         nc.tensor.matmul(gains[:, 0, :], lhsT=ones_row[:], rhs=fn_row[:], start=True, stop=True)
@@ -214,7 +211,9 @@ def tile_crossattention_pa_t_kernel(tc, features, fn_w, Wk_w, Wk_b, kn_w, out):
             turned[pair] = turn(normed, pair)
         nc.tensor.matmul(gains[:, 1, :], lhsT=ones_row[:], rhs=other_rows[:, 0, :], start=True, stop=True)
         quantise(w_grouped, w_codes, w_scales)
-        bias = spread_vector(1)
+        bias = const.tile([P, D], F32)
+        spread_vector(1, bias[:])
+        kn_gain_sbuf = const.tile([P, SLOTS, D], F32)
 
         products, biased = {}, {}
         for i in range(GROUPS):
@@ -249,7 +248,11 @@ def tile_crossattention_pa_t_kernel(tc, features, fn_w, Wk_w, Wk_b, kn_w, out):
             if i + 2 < GROUPS or i >= 1:
                 rms = root(totals, 0 if i + 2 < GROUPS else SLOTS, 2 * SLOTS if i >= 1 else SLOTS)
             if i == 1:
-                kn_gain_sbuf = spread_vector(0)
+                spread_vector(0, kn_gain_sbuf[:, 0, :])
+                for s in range(1, -(-GPSIMD_COLUMNS // D)):
+                    nc.gpsimd.tensor_scalar(
+                        out=kn_gain_sbuf[:, s, :], in0=kn_gain_sbuf[:, 0, :], scalar1=1.0, scalar2=0.0, op0=ALU.mult, op1=ALU.add
+                    )
             if i == 0:
                 grouped = next_grouped
             elif i + 1 < GROUPS:
@@ -273,5 +276,5 @@ def tile_crossattention_pa_t_kernel(tc, features, fn_w, Wk_w, Wk_b, kn_w, out):
         for pair in range(PAIRS):
             inverse = invert(roots[pair], 2 * pair, 2 * pair + 2)
             for s in (2 * pair, 2 * pair + 1):
-                vector_finish(last, s, inverse[:, s : s + 1])
+                vector_finish(last, s, 0, inverse[:, s : s + 1])
                 nc.sync.dma_start(out=out_dram[GROUPS - 1, :, s, :], in_=last[:, s, :])

@@ -42,8 +42,8 @@ def tile_crossattention_pa_t_kernel(tc, features, fn_w, Wk_w, Wk_b, kn_w, out):
         make_identity(nc, ident[:])
         fn_row = const.tile([P, D], BF16)
         nc.vector.memset(fn_row[:], 0.0)
-        other_rows = const.tile([P, 2, D], BF16)
-        nc.gpsimd.memset(other_rows[:], 0.0)
+        kn_row = const.tile([P, D], BF16)
+        nc.gpsimd.memset(kn_row[:], 0.0)
         ones_row = const.tile([P, P], BF16)
         nc.vector.memset(ones_row[:], 0.0)
         nc.vector.memset(ones_row[0:1, :], 1.0)
@@ -51,6 +51,8 @@ def tile_crossattention_pa_t_kernel(tc, features, fn_w, Wk_w, Wk_b, kn_w, out):
         def load_row(row, source):
             nc.sync.dma_start(out=row, in_=source.rearrange("(a d) -> a d", a=1))
 
+        bias = const.tile([P, D], BF16)
+        kn_gain_sbuf = const.tile([P, SLOTS, D], BF16)
         x_rows = []
         w_rows = const.tile([P, SLOTS, D], BF16)
         for g in range(GROUPS):
@@ -59,14 +61,16 @@ def tile_crossattention_pa_t_kernel(tc, features, fn_w, Wk_w, Wk_b, kn_w, out):
             if g == 0:
                 for s in range(SLOTS):
                     nc.sync.dma_start(out=x_g[:, s, :], in_=x_dram[g, :, s, :])
-                    if s == 0:
+                    if s == 1:
                         load_row(fn_row[0:1, :], fn_w)
             else:
                 nc.sync.dma_start(out=x_g[:], in_=x_dram[g])
             if g == 1:
                 nc.sync.dma_start(out=w_rows[:], in_=Wk_w.rearrange("(s p) k -> p s k", p=P))
-                load_row(other_rows[0:1, 0, :], kn_w)
-                load_row(other_rows[0:1, 1, :], Wk_b)
+                load_row(kn_row[0:1, :], kn_w)
+                nc.sync.dma_start(out=bias[:], in_=Wk_b.partition_broadcast(P))
+            if g == 2:
+                nc.sync.dma_start(out=kn_gain_sbuf[:, 0, :], in_=kn_w.partition_broadcast(P))
 
         def scalar_square_sum(row, total):
             squares = small.tile([P, D], BF16)
@@ -166,11 +170,6 @@ def tile_crossattention_pa_t_kernel(tc, features, fn_w, Wk_w, Wk_b, kn_w, out):
             queue = nc.scalar if g == GROUPS - 2 else nc.sync
             queue.dma_start(out=out_dram[g], in_=biased[:])
 
-        def spread_vector(v, copy):
-            bank = turned_banks.tile([P, D], F32, name="turned")
-            nc.tensor.matmul(bank[:], lhsT=ones_row[:], rhs=other_rows[:, v, :], start=True, stop=True)
-            nc.scalar.copy(out=copy, in_=bank[:])
-
         gains = gain_bank.tile([P, 2, D], BF16)
         nc.tensor.matmul(gains[:, 0, :], lhsT=ones_row[:], rhs=fn_row[:], start=True, stop=True)
         totals = small.tile([P, 2 * SLOTS], F32, name="totals")
@@ -191,8 +190,9 @@ def tile_crossattention_pa_t_kernel(tc, features, fn_w, Wk_w, Wk_b, kn_w, out):
         turned[1] = turn(normed, 1)
 
         totals = small.tile([P, 2 * SLOTS], F32, name="totals")
-        for s in range(SLOTS):
+        for s in (0, 1, 2):
             scalar_square_sum(x_rows[1][:, s, :], totals[:, s : s + 1])
+        vector_square_sum(x_rows[1][:, 3, :], totals[:, 3:4])
         rms = root(totals, 0, SLOTS)
         grouped = work.tile([P, SLOTS, P, PACK], BF16, align_bytes=64, name="grouped")
         for pair in range(PAIRS):
@@ -209,11 +209,8 @@ def tile_crossattention_pa_t_kernel(tc, features, fn_w, Wk_w, Wk_b, kn_w, out):
             for s in (2 * pair, 2 * pair + 1):
                 normalise(1, s, inverse, normed)
             turned[pair] = turn(normed, pair)
-        nc.tensor.matmul(gains[:, 1, :], lhsT=ones_row[:], rhs=other_rows[:, 0, :], start=True, stop=True)
+        nc.tensor.matmul(gains[:, 1, :], lhsT=ones_row[:], rhs=kn_row[:], start=True, stop=True)
         quantise(w_grouped, w_codes, w_scales)
-        bias = const.tile([P, D], F32)
-        spread_vector(1, bias[:])
-        kn_gain_sbuf = const.tile([P, SLOTS, D], F32)
 
         products, biased = {}, {}
         for i in range(GROUPS):
@@ -227,7 +224,7 @@ def tile_crossattention_pa_t_kernel(tc, features, fn_w, Wk_w, Wk_b, kn_w, out):
             if i >= 1:
                 biased[i - 1] = result.tile([P, SLOTS, D], F32, name="biased")
             for s in range(SLOTS):
-                if i + 2 < GROUPS and not (i == 0 and s >= 2):
+                if i + 2 < GROUPS and not (i <= 1 and s >= 2):
                     scalar_square_sum(x_rows[i + 2][:, s, :], totals[:, s : s + 1])
                 if i >= 2 and s == 0:
                     regroup(turned[1], 1, grouped)
@@ -238,17 +235,14 @@ def tile_crossattention_pa_t_kernel(tc, features, fn_w, Wk_w, Wk_b, kn_w, out):
                     quantise(grouped, codes, scales)
                     if i >= 1:
                         inverse = invert(rms, 0 if i + 1 < GROUPS else SLOTS, 2 * SLOTS if i >= 2 else SLOTS)
-            if i == 0:
+            if i <= 1:
                 for s in (2, 3):
-                    vector_square_sum(x_rows[2][:, s, :], totals[:, s : s + 1])
+                    vector_square_sum(x_rows[i + 2][:, s, :], totals[:, s : s + 1])
             if i >= 2:
                 finish(i - 2, biased[i - 2], inverse)
             for s in range(SLOTS):
                 products[s] = multiply(codes, scales, s)
-            if i + 2 < GROUPS or i >= 1:
-                rms = root(totals, 0 if i + 2 < GROUPS else SLOTS, 2 * SLOTS if i >= 1 else SLOTS)
-            if i == 1:
-                spread_vector(0, kn_gain_sbuf[:, 0, :])
+            if i == 0:
                 for s in range(1, -(-GPSIMD_COLUMNS // D)):
                     nc.gpsimd.tensor_scalar(
                         out=kn_gain_sbuf[:, s, :], in0=kn_gain_sbuf[:, 0, :], scalar1=1.0, scalar2=0.0, op0=ALU.mult, op1=ALU.add
@@ -263,6 +257,7 @@ def tile_crossattention_pa_t_kernel(tc, features, fn_w, Wk_w, Wk_b, kn_w, out):
                     turned[pair] = turn(normed, pair)
                 grouped = work.tile([P, SLOTS, P, PACK], BF16, align_bytes=64, name="grouped")
                 regroup(turned[0], 0, grouped)
+            rms = root(totals, 0 if i + 2 < GROUPS else SLOTS, 2 * SLOTS if i >= 1 else SLOTS)
 
         last = result.tile([P, SLOTS, D], F32, name="biased")
         totals = small.tile([P, 2 * SLOTS], F32, name="totals")

@@ -44,6 +44,8 @@ def tile_crossattention_pa_t_kernel(tc, features, fn_w, Wk_w, Wk_b, kn_w, out):
         nc.vector.memset(fn_row[:], 0.0)
         kn_row = const.tile([P, D], BF16)
         nc.gpsimd.memset(kn_row[:], 0.0)
+        bias_row = const.tile([P, D], BF16)
+        nc.gpsimd.memset(bias_row[:], 0.0)
         ones_row = const.tile([P, P], BF16)
         nc.vector.memset(ones_row[:], 0.0)
         nc.vector.memset(ones_row[0:1, :], 1.0)
@@ -51,7 +53,6 @@ def tile_crossattention_pa_t_kernel(tc, features, fn_w, Wk_w, Wk_b, kn_w, out):
         def load_row(row, source):
             nc.sync.dma_start(out=row, in_=source.rearrange("(a d) -> a d", a=1))
 
-        bias = const.tile([P, D], BF16)
         kn_gain_sbuf = const.tile([P, SLOTS, D], BF16)
         x_rows = []
         w_rows = const.tile([P, SLOTS, D], BF16)
@@ -68,8 +69,8 @@ def tile_crossattention_pa_t_kernel(tc, features, fn_w, Wk_w, Wk_b, kn_w, out):
             if g == 1:
                 nc.sync.dma_start(out=w_rows[:], in_=Wk_w.rearrange("(s p) k -> p s k", p=P))
                 load_row(kn_row[0:1, :], kn_w)
-                nc.sync.dma_start(out=bias[:], in_=Wk_b.partition_broadcast(P))
-            if g == 2:
+                load_row(bias_row[0:1, :], Wk_b)
+            if g == 5:
                 nc.sync.dma_start(out=kn_gain_sbuf[:, 0, :], in_=kn_w.partition_broadcast(P))
 
         def scalar_square_sum(row, total):
@@ -202,6 +203,10 @@ def tile_crossattention_pa_t_kernel(tc, features, fn_w, Wk_w, Wk_b, kn_w, out):
         w_grouped = const.tile([P, SLOTS, P, PACK], BF16, align_bytes=64)
         for pair in range(PAIRS):
             regroup(turn(w_rows, pair), pair, w_grouped)
+        bias = const.tile([P, D], F32)
+        bias_bank = turned_banks.tile([P, D], F32, name="turned")
+        nc.tensor.matmul(bias_bank[:], lhsT=ones_row[:], rhs=bias_row[:], start=True, stop=True)
+        nc.scalar.copy(out=bias[:], in_=bias_bank[:])
 
         inverse = invert(rms, 0, SLOTS)
         normed = work.tile([P, SLOTS, D], BF16, name="normed")
@@ -224,7 +229,7 @@ def tile_crossattention_pa_t_kernel(tc, features, fn_w, Wk_w, Wk_b, kn_w, out):
             if i >= 1:
                 biased[i - 1] = result.tile([P, SLOTS, D], F32, name="biased")
             for s in range(SLOTS):
-                if i + 2 < GROUPS and not (i <= 1 and s >= 2):
+                if i + 2 < GROUPS and not (i == 0 and s >= 2):
                     scalar_square_sum(x_rows[i + 2][:, s, :], totals[:, s : s + 1])
                 if i >= 2 and s == 0:
                     regroup(turned[1], 1, grouped)
@@ -235,9 +240,9 @@ def tile_crossattention_pa_t_kernel(tc, features, fn_w, Wk_w, Wk_b, kn_w, out):
                     quantise(grouped, codes, scales)
                     if i >= 1:
                         inverse = invert(rms, 0 if i + 1 < GROUPS else SLOTS, 2 * SLOTS if i >= 2 else SLOTS)
-            if i <= 1:
+            if i == 0:
                 for s in (2, 3):
-                    vector_square_sum(x_rows[i + 2][:, s, :], totals[:, s : s + 1])
+                    vector_square_sum(x_rows[2][:, s, :], totals[:, s : s + 1])
             if i >= 2:
                 finish(i - 2, biased[i - 2], inverse)
             for s in range(SLOTS):

@@ -60,9 +60,10 @@ def tile_crossattention_pa_t_kernel(tc, features, fn_w, Wk_w, Wk_b, kn_w, out):
             x_g = resident.tile([P, SLOTS, D], BF16, name="x%d" % g)
             x_rows.append(x_g)
             if g == 0:
-                for s in range(SLOTS):
-                    nc.sync.dma_start(out=x_g[:, s, :], in_=x_dram[g, :, s, :])
-                    if s == 1:
+                for pair in range(PAIRS):
+                    slots = slice(2 * pair, 2 * pair + 2)
+                    nc.sync.dma_start(out=x_g[:, slots, :], in_=x_dram[g, :, slots, :])
+                    if pair == 0:
                         load_row(fn_row[0:1, :], fn_w)
             else:
                 nc.sync.dma_start(out=x_g[:], in_=x_dram[g])
@@ -168,32 +169,31 @@ def tile_crossattention_pa_t_kernel(tc, features, fn_w, Wk_w, Wk_b, kn_w, out):
             flat = biased[:].rearrange("p s o -> p (s o)")[:, :shared]
             kn_flat = kn_gain_sbuf[:].rearrange("p s o -> p (s o)")[:, :shared]
             nc.gpsimd.tensor_tensor(out=flat, in0=flat, in1=kn_flat, op=ALU.mult)
-            queue = nc.scalar if g == GROUPS - 2 else nc.sync
-            queue.dma_start(out=out_dram[g], in_=biased[:])
+            if g < GROUPS - 2:
+                nc.sync.dma_start(out=out_dram[g], in_=biased[:])
+            else:
+                nc.sync.dma_start(out=out_dram[g, :, 1:, :], in_=biased[:, 1:, :])
+                nc.scalar.dma_start(out=out_dram[g, :, 0, :], in_=biased[:, 0, :])
 
         gains = gain_bank.tile([P, 2, D], BF16)
         nc.tensor.matmul(gains[:, 0, :], lhsT=ones_row[:], rhs=fn_row[:], start=True, stop=True)
         totals = small.tile([P, 2 * SLOTS], F32, name="totals")
         normed = work.tile([P, SLOTS, D], BF16, name="normed")
         turned = {}
-        scalar_square_sum(x_rows[0][:, 0, :], totals[:, 0:1])
-        vector_square_sum(x_rows[0][:, 1, :], totals[:, 1:2])
-        inverse = invert(root(totals, 0, 2), 0, 2)
-        for s in (2, 3):
-            scalar_square_sum(x_rows[0][:, s, :], totals[:, s : s + 1])
-        rms = root(totals, 2, SLOTS)
-        for s in (0, 1):
-            normalise(0, s, inverse, normed)
-        turned[0] = turn(normed, 0)
-        inverse = invert(rms, 2, SLOTS)
-        for s in (2, 3):
-            normalise(0, s, inverse, normed)
-        turned[1] = turn(normed, 1)
+        roots = []
+        for pair in range(PAIRS):
+            scalar_square_sum(x_rows[0][:, 2 * pair, :], totals[:, 2 * pair : 2 * pair + 1])
+            vector_square_sum(x_rows[0][:, 2 * pair + 1, :], totals[:, 2 * pair + 1 : 2 * pair + 2])
+            roots.append(root(totals, 2 * pair, 2 * pair + 2))
+        for pair in range(PAIRS):
+            inverse = invert(roots[pair], 2 * pair, 2 * pair + 2)
+            for s in (2 * pair, 2 * pair + 1):
+                normalise(0, s, inverse, normed)
+            turned[pair] = turn(normed, pair)
 
         totals = small.tile([P, 2 * SLOTS], F32, name="totals")
-        for s in (0, 1, 2):
+        for s in range(SLOTS):
             scalar_square_sum(x_rows[1][:, s, :], totals[:, s : s + 1])
-        vector_square_sum(x_rows[1][:, 3, :], totals[:, 3:4])
         rms = root(totals, 0, SLOTS)
         grouped = work.tile([P, SLOTS, P, PACK], BF16, align_bytes=64, name="grouped")
         for pair in range(PAIRS):
@@ -214,7 +214,6 @@ def tile_crossattention_pa_t_kernel(tc, features, fn_w, Wk_w, Wk_b, kn_w, out):
             for s in (2 * pair, 2 * pair + 1):
                 normalise(1, s, inverse, normed)
             turned[pair] = turn(normed, pair)
-        nc.tensor.matmul(gains[:, 1, :], lhsT=ones_row[:], rhs=kn_row[:], start=True, stop=True)
         quantise(w_grouped, w_codes, w_scales)
 
         products, biased = {}, {}
@@ -248,6 +247,7 @@ def tile_crossattention_pa_t_kernel(tc, features, fn_w, Wk_w, Wk_b, kn_w, out):
             for s in range(SLOTS):
                 products[s] = multiply(codes, scales, s)
             if i == 0:
+                nc.tensor.matmul(gains[:, 1, :], lhsT=ones_row[:], rhs=kn_row[:], start=True, stop=True)
                 for s in range(1, -(-GPSIMD_COLUMNS // D)):
                     nc.gpsimd.tensor_scalar(
                         out=kn_gain_sbuf[:, s, :], in0=kn_gain_sbuf[:, 0, :], scalar1=1.0, scalar2=0.0, op0=ALU.mult, op1=ALU.add

@@ -29,7 +29,7 @@ def tile_crossattention_pa_t_kernel(tc, features, fn_w, Wk_w, Wk_b, kn_w, out):
 
     with tc.tile_pool(name="const", bufs=1) as const, tc.tile_pool(name="resident", bufs=1) as resident, tc.tile_pool(
         name="work", bufs=2
-    ) as work, tc.tile_pool(name="result", bufs=6) as result, tc.tile_pool(name="small", bufs=4) as small, tc.psum_pool(
+    ) as work, tc.tile_pool(name="sums", bufs=3) as sums, tc.tile_pool(name="result", bufs=5) as result, tc.tile_pool(name="small", bufs=4) as small, tc.psum_pool(
         name="turned_banks", bufs=3
     ) as turned_banks, tc.psum_pool(name="product_banks", bufs=4) as product_banks, tc.psum_pool(
         name="gain_bank", bufs=1
@@ -141,9 +141,9 @@ def tile_crossattention_pa_t_kernel(tc, features, fn_w, Wk_w, Wk_b, kn_w, out):
         def add_bias(product, biased, s):
             nc.vector.tensor_tensor(out=biased[:, s, :], in0=product[:], in1=bias[:], op=ALU.add)
 
-        def vector_finish(biased, s, first, inverse):
+        def vector_finish(biased, finished, s, first, inverse):
             nc.vector.scalar_tensor_tensor(
-                out=biased[:, s, first:],
+                out=finished[:, s, first:],
                 in0=biased[:, s, first:],
                 scalar=inverse,
                 in1=gains[:, 1, first:],
@@ -151,29 +151,40 @@ def tile_crossattention_pa_t_kernel(tc, features, fn_w, Wk_w, Wk_b, kn_w, out):
                 op1=ALU.mult,
             )
 
-        def finish(g, biased, inverse):
-            shared = min(GPSIMD_COLUMNS, (GROUPS - 1 - g) * D)
+        def gpsimd_columns(g):
+            return min(GPSIMD_COLUMNS, (GROUPS - 1 - g) * D)
+
+        def gain_shared(g, biased):
+            finished = result.tile([P, SLOTS, D], F32, name="finished")
+            shared = gpsimd_columns(g)
+            nc.gpsimd.tensor_tensor(
+                out=finished[:].rearrange("p s o -> p (s o)")[:, :shared],
+                in0=biased[:].rearrange("p s o -> p (s o)")[:, :shared],
+                in1=kn_gain_sbuf[:].rearrange("p s o -> p (s o)")[:, :shared],
+                op=ALU.mult,
+            )
+            return finished
+
+        def finish(g, biased, finished, inverse):
+            shared = gpsimd_columns(g)
             for s in range(SLOTS):
                 ours = min(max(shared - s * D, 0), D)
                 if ours > 0:
                     nc.gpsimd.tensor_scalar(
-                        out=biased[:, s, :ours],
-                        in0=biased[:, s, :ours],
+                        out=finished[:, s, :ours],
+                        in0=finished[:, s, :ours],
                         scalar1=inverse[:, SLOTS + s : SLOTS + s + 1],
                         scalar2=0.0,
                         op0=ALU.mult,
                         op1=ALU.add,
                     )
                 if ours < D:
-                    vector_finish(biased, s, ours, inverse[:, SLOTS + s : SLOTS + s + 1])
-            flat = biased[:].rearrange("p s o -> p (s o)")[:, :shared]
-            kn_flat = kn_gain_sbuf[:].rearrange("p s o -> p (s o)")[:, :shared]
-            nc.gpsimd.tensor_tensor(out=flat, in0=flat, in1=kn_flat, op=ALU.mult)
+                    vector_finish(biased, finished, s, ours, inverse[:, SLOTS + s : SLOTS + s + 1])
             if g < GROUPS - 2:
-                nc.sync.dma_start(out=out_dram[g], in_=biased[:])
+                nc.sync.dma_start(out=out_dram[g], in_=finished[:])
             else:
-                nc.sync.dma_start(out=out_dram[g, :, 1:, :], in_=biased[:, 1:, :])
-                nc.scalar.dma_start(out=out_dram[g, :, 0, :], in_=biased[:, 0, :])
+                nc.sync.dma_start(out=out_dram[g, :, 1:, :], in_=finished[:, 1:, :])
+                nc.scalar.dma_start(out=out_dram[g, :, 0, :], in_=finished[:, 0, :])
 
         gains = gain_bank.tile([P, 2, D], BF16)
         nc.tensor.matmul(gains[:, 0, :], lhsT=ones_row[:], rhs=fn_row[:], start=True, stop=True)
@@ -216,7 +227,7 @@ def tile_crossattention_pa_t_kernel(tc, features, fn_w, Wk_w, Wk_b, kn_w, out):
             turned[pair] = turn(normed, pair)
         quantise(w_grouped, w_codes, w_scales)
 
-        products, biased = {}, {}
+        products, biased, finished = {}, {}, {}
         for i in range(GROUPS):
             totals = small.tile([P, 2 * SLOTS], F32, name="totals")
             if i == 0:
@@ -226,7 +237,7 @@ def tile_crossattention_pa_t_kernel(tc, features, fn_w, Wk_w, Wk_b, kn_w, out):
             codes = work.tile([P, SLOTS * P], U32, align_bytes=64)
             scales = work.tile([P, SLOTS * P], U8, align_bytes=64)
             if i >= 1:
-                biased[i - 1] = result.tile([P, SLOTS, D], F32, name="biased")
+                biased[i - 1] = sums.tile([P, SLOTS, D], F32, name="biased")
             for s in range(SLOTS):
                 if i + 2 < GROUPS and not (i == 0 and s >= 2):
                     scalar_square_sum(x_rows[i + 2][:, s, :], totals[:, s : s + 1])
@@ -243,7 +254,9 @@ def tile_crossattention_pa_t_kernel(tc, features, fn_w, Wk_w, Wk_b, kn_w, out):
                 for s in (2, 3):
                     vector_square_sum(x_rows[2][:, s, :], totals[:, s : s + 1])
             if i >= 2:
-                finish(i - 2, biased[i - 2], inverse)
+                finish(i - 2, biased[i - 2], finished[i - 2], inverse)
+            if i >= 1:
+                finished[i - 1] = gain_shared(i - 1, biased[i - 1])
             for s in range(SLOTS):
                 products[s] = multiply(codes, scales, s)
             if i == 0:
@@ -264,7 +277,7 @@ def tile_crossattention_pa_t_kernel(tc, features, fn_w, Wk_w, Wk_b, kn_w, out):
                 regroup(turned[0], 0, grouped)
             rms = root(totals, 0 if i + 2 < GROUPS else SLOTS, 2 * SLOTS if i >= 1 else SLOTS)
 
-        last = result.tile([P, SLOTS, D], F32, name="biased")
+        last = sums.tile([P, SLOTS, D], F32, name="biased")
         totals = small.tile([P, 2 * SLOTS], F32, name="totals")
         roots = []
         for pair in range(PAIRS):
@@ -272,9 +285,9 @@ def tile_crossattention_pa_t_kernel(tc, features, fn_w, Wk_w, Wk_b, kn_w, out):
                 add_bias(products[s], last, s)
                 scalar_square_sum(last[:, s, :], totals[:, s : s + 1])
             roots.append(root(totals, 2 * pair, 2 * pair + 2))
-        finish(GROUPS - 2, biased[GROUPS - 2], invert(rms, SLOTS, 2 * SLOTS))
+        finish(GROUPS - 2, biased[GROUPS - 2], finished[GROUPS - 2], invert(rms, SLOTS, 2 * SLOTS))
         for pair in range(PAIRS):
             inverse = invert(roots[pair], 2 * pair, 2 * pair + 2)
             for s in (2 * pair, 2 * pair + 1):
-                vector_finish(last, s, 0, inverse[:, s : s + 1])
+                vector_finish(last, last, s, 0, inverse[:, s : s + 1])
                 nc.sync.dma_start(out=out_dram[GROUPS - 1, :, s, :], in_=last[:, s, :])

@@ -37,7 +37,7 @@ def tile_crossattention_pa_t_kernel(tc, features, fn_w, Wk_w, Wk_b, kn_w, out):
         eps = const.tile([P, 1], F32)
         nc.vector.memset(eps[:], EPS)
         warm = const.tile([P, 1], F32)
-        nc.scalar.activation(out=warm[:], in_=eps[:], func=ACT.Sqrt)
+        nc.scalar.activation(out=warm[:], in_=eps[:], func=ACT.Abs_reciprocal_sqrt)
         ident = const.tile([P, P], F32)
         make_identity(nc, ident[:])
         fn_row = const.tile([P, D], BF16)
@@ -84,17 +84,21 @@ def tile_crossattention_pa_t_kernel(tc, features, fn_w, Wk_w, Wk_b, kn_w, out):
                 out=products[:], in0=row, scalar=1.0, in1=row, op0=ALU.mult, op1=ALU.mult, accum_out=total
             )
 
-        def root(totals, first, last):
-            rms = small.tile([P, 2 * SLOTS], F32)
-            nc.scalar.activation(
-                out=rms[:, first:last], in_=totals[:, first:last], func=ACT.Sqrt, scale=1.0 / D, bias=eps[:]
-            )
-            return rms
-
-        def invert(rms, first, last):
+        def inverse_root(totals, first, last):
             inverse = small.tile([P, 2 * SLOTS], F32)
-            nc.vector.reciprocal(out=inverse[:, first:last], in_=rms[:, first:last])
+            nc.scalar.activation(
+                out=inverse[:, first:last],
+                in_=totals[:, first:last],
+                func=ACT.Abs_reciprocal_sqrt,
+                scale=1.0 / D,
+                bias=eps[:],
+            )
             return inverse
+
+        def release(inverse):
+            released = small.tile([P, SLOTS], F32)
+            nc.vector.tensor_copy(out=released[:], in_=inverse[:, SLOTS:])
+            return released
 
         def normalise(g, s, inverse, normed):
             nc.vector.scalar_tensor_tensor(
@@ -165,7 +169,7 @@ def tile_crossattention_pa_t_kernel(tc, features, fn_w, Wk_w, Wk_b, kn_w, out):
             )
             return finished
 
-        def finish(g, biased, finished, inverse):
+        def finish(g, biased, finished, inverse, released):
             shared = gpsimd_columns(g)
             for s in range(SLOTS):
                 ours = min(max(shared - s * D, 0), D)
@@ -173,7 +177,7 @@ def tile_crossattention_pa_t_kernel(tc, features, fn_w, Wk_w, Wk_b, kn_w, out):
                     nc.gpsimd.tensor_scalar(
                         out=finished[:, s, :ours],
                         in0=finished[:, s, :ours],
-                        scalar1=inverse[:, SLOTS + s : SLOTS + s + 1],
+                        scalar1=released[:, s : s + 1],
                         scalar2=0.0,
                         op0=ALU.mult,
                         op1=ALU.add,
@@ -191,21 +195,20 @@ def tile_crossattention_pa_t_kernel(tc, features, fn_w, Wk_w, Wk_b, kn_w, out):
         totals = small.tile([P, 2 * SLOTS], F32, name="totals")
         normed = work.tile([P, SLOTS, D], BF16, name="normed")
         turned = {}
-        roots = []
+        inverses = []
         for pair in range(PAIRS):
             scalar_square_sum(x_rows[0][:, 2 * pair, :], totals[:, 2 * pair : 2 * pair + 1])
             vector_square_sum(x_rows[0][:, 2 * pair + 1, :], totals[:, 2 * pair + 1 : 2 * pair + 2])
-            roots.append(root(totals, 2 * pair, 2 * pair + 2))
+            inverses.append(inverse_root(totals, 2 * pair, 2 * pair + 2))
         for pair in range(PAIRS):
-            inverse = invert(roots[pair], 2 * pair, 2 * pair + 2)
             for s in (2 * pair, 2 * pair + 1):
-                normalise(0, s, inverse, normed)
+                normalise(0, s, inverses[pair], normed)
             turned[pair] = turn(normed, pair)
 
         totals = small.tile([P, 2 * SLOTS], F32, name="totals")
         for s in range(SLOTS):
             scalar_square_sum(x_rows[1][:, s, :], totals[:, s : s + 1])
-        rms = root(totals, 0, SLOTS)
+        inverse = inverse_root(totals, 0, SLOTS)
         grouped = work.tile([P, SLOTS, P, PACK], BF16, align_bytes=64, name="grouped")
         for pair in range(PAIRS):
             regroup(turned[pair], pair, grouped)
@@ -219,7 +222,6 @@ def tile_crossattention_pa_t_kernel(tc, features, fn_w, Wk_w, Wk_b, kn_w, out):
         nc.tensor.matmul(bias_bank[:], lhsT=ones_row[:], rhs=bias_row[:], start=True, stop=True)
         nc.scalar.copy(out=bias[:], in_=bias_bank[:])
 
-        inverse = invert(rms, 0, SLOTS)
         normed = work.tile([P, SLOTS, D], BF16, name="normed")
         for pair in range(PAIRS):
             for s in (2 * pair, 2 * pair + 1):
@@ -248,13 +250,13 @@ def tile_crossattention_pa_t_kernel(tc, features, fn_w, Wk_w, Wk_b, kn_w, out):
                     scalar_square_sum(biased[i - 1][:, s, :], totals[:, SLOTS + s : SLOTS + s + 1])
                 if s == (2 if i + 1 < GROUPS else 1):
                     quantise(grouped, codes, scales)
-                    if i >= 1:
-                        inverse = invert(rms, 0 if i + 1 < GROUPS else SLOTS, 2 * SLOTS if i >= 2 else SLOTS)
+                    if i >= 2:
+                        released = release(inverse)
             if i == 0:
                 for s in (2, 3):
                     vector_square_sum(x_rows[2][:, s, :], totals[:, s : s + 1])
             if i >= 2:
-                finish(i - 2, biased[i - 2], finished[i - 2], inverse)
+                finish(i - 2, biased[i - 2], finished[i - 2], inverse, released)
             if i >= 1:
                 finished[i - 1] = gain_shared(i - 1, biased[i - 1])
             for s in range(SLOTS):
@@ -275,19 +277,18 @@ def tile_crossattention_pa_t_kernel(tc, features, fn_w, Wk_w, Wk_b, kn_w, out):
                     turned[pair] = turn(normed, pair)
                 grouped = work.tile([P, SLOTS, P, PACK], BF16, align_bytes=64, name="grouped")
                 regroup(turned[0], 0, grouped)
-            rms = root(totals, 0 if i + 2 < GROUPS else SLOTS, 2 * SLOTS if i >= 1 else SLOTS)
+            inverse = inverse_root(totals, 0 if i + 2 < GROUPS else SLOTS, 2 * SLOTS if i >= 1 else SLOTS)
 
         last = sums.tile([P, SLOTS, D], F32, name="biased")
         totals = small.tile([P, 2 * SLOTS], F32, name="totals")
-        roots = []
+        inverses = []
         for pair in range(PAIRS):
             for s in (2 * pair, 2 * pair + 1):
                 add_bias(products[s], last, s)
                 scalar_square_sum(last[:, s, :], totals[:, s : s + 1])
-            roots.append(root(totals, 2 * pair, 2 * pair + 2))
-        finish(GROUPS - 2, biased[GROUPS - 2], finished[GROUPS - 2], invert(rms, SLOTS, 2 * SLOTS))
+            inverses.append(inverse_root(totals, 2 * pair, 2 * pair + 2))
+        finish(GROUPS - 2, biased[GROUPS - 2], finished[GROUPS - 2], inverse, inverse[:, SLOTS:])
         for pair in range(PAIRS):
-            inverse = invert(roots[pair], 2 * pair, 2 * pair + 2)
             for s in (2 * pair, 2 * pair + 1):
-                vector_finish(last, last, s, 0, inverse[:, s : s + 1])
+                vector_finish(last, last, s, 0, inverses[pair][:, s : s + 1])
                 nc.sync.dma_start(out=out_dram[GROUPS - 1, :, s, :], in_=last[:, s, :])

@@ -19,6 +19,9 @@ GROUPS = TOKENS // (P * SLOTS)
 EPS = 1e-6
 GPSIMD_COLUMNS = 2 * D + D // 2
 
+LAST_COLUMNS = {GROUPS - 3: 3 * D, GROUPS - 2: 2 * D}
+SCALAR_SLOTS = {GROUPS - 4: (1, 2), GROUPS - 3: (2,), GROUPS - 2: (0, 1)}
+
 FLOPS = 2 * TOKENS * D * D
 
 
@@ -110,16 +113,16 @@ def tile_crossattention_pa_t_kernel(tc, features, fn_w, Wk_w, Wk_b, kn_w, out):
                 op1=ALU.mult,
             )
 
-        def turn(rows, pair):
-            turned = turned_banks.tile([P, 2, 2, P], F32)
+        def turn(rows, pair, pool=turned_banks, name="turned"):
+            turned = pool.tile([P, 2, 2, P], F32, name=name)
             for s in range(2):
                 words = rows[:, 2 * pair + s, :].bitcast(F32)
                 for u in range(2):
                     nc.tensor.transpose(turned[:, s, u, :], words[:, u : D // 2 : 2], ident[:])
             return turned
 
-        def regroup(turned, pair, grouped):
-            nc.scalar.copy(
+        def regroup(turned, pair, grouped, copy=nc.scalar.copy):
+            copy(
                 out=grouped[:, 2 * pair : 2 * pair + 2, :, :].rearrange("p s r t -> p (s r t)").bitcast(F32),
                 in_=turned[:].rearrange("p s u r -> p s r u"),
             )
@@ -130,7 +133,7 @@ def tile_crossattention_pa_t_kernel(tc, features, fn_w, Wk_w, Wk_b, kn_w, out):
             )
 
         def multiply(codes, scales, s):
-            product = product_banks.tile([P, D], F32)
+            product = product_banks.tile([P, D], F32, name="product")
             nc.tensor.matmul_mx(
                 out=product[:],
                 lhsT=codes[:, s * P : (s + 1) * P].bitcast(FP8X4),
@@ -156,7 +159,16 @@ def tile_crossattention_pa_t_kernel(tc, features, fn_w, Wk_w, Wk_b, kn_w, out):
             )
 
         def gpsimd_columns(g):
-            return min(GPSIMD_COLUMNS, (GROUPS - 1 - g) * D)
+            return LAST_COLUMNS.get(g, GPSIMD_COLUMNS)
+
+        def slot_columns(g, s):
+            return min(max(gpsimd_columns(g) - s * D, 0), D)
+
+        def scalar_scale(g, s, inverse):
+            ours = slot_columns(g, s)
+            nc.scalar.activation(
+                out=finished[g][:, s, :ours], in_=finished[g][:, s, :ours], func=ACT.Copy, scale=inverse
+            )
 
         def gain_shared(g, biased):
             finished = result.tile([P, SLOTS, D], F32, name="finished")
@@ -170,10 +182,9 @@ def tile_crossattention_pa_t_kernel(tc, features, fn_w, Wk_w, Wk_b, kn_w, out):
             return finished
 
         def finish(g, biased, finished, inverse, released):
-            shared = gpsimd_columns(g)
             for s in range(SLOTS):
-                ours = min(max(shared - s * D, 0), D)
-                if ours > 0:
+                ours = slot_columns(g, s)
+                if ours > 0 and s not in SCALAR_SLOTS.get(g, ()):
                     nc.gpsimd.tensor_scalar(
                         out=finished[:, s, :ours],
                         in0=finished[:, s, :ours],
@@ -187,8 +198,8 @@ def tile_crossattention_pa_t_kernel(tc, features, fn_w, Wk_w, Wk_b, kn_w, out):
             if g < GROUPS - 2:
                 nc.sync.dma_start(out=out_dram[g], in_=finished[:])
             else:
-                nc.sync.dma_start(out=out_dram[g, :, 1:, :], in_=finished[:, 1:, :])
-                nc.scalar.dma_start(out=out_dram[g, :, 0, :], in_=finished[:, 0, :])
+                first = len(SCALAR_SLOTS[g])
+                nc.sync.dma_start(out=out_dram[g, :, first:, :], in_=finished[:, first:, :])
 
         gains = gain_bank.tile([P, 2, D], BF16)
         nc.tensor.matmul(gains[:, 0, :], lhsT=ones_row[:], rhs=fn_row[:], start=True, stop=True)
@@ -206,19 +217,21 @@ def tile_crossattention_pa_t_kernel(tc, features, fn_w, Wk_w, Wk_b, kn_w, out):
             turned[pair] = turn(normed, pair)
 
         totals = small.tile([P, 2 * SLOTS], F32, name="totals")
-        for s in range(SLOTS):
+        for s in range(3):
             scalar_square_sum(x_rows[1][:, s, :], totals[:, s : s + 1])
-        inverse = inverse_root(totals, 0, SLOTS)
+        for s in range(3, SLOTS):
+            vector_square_sum(x_rows[1][:, s, :], totals[:, s : s + 1])
         grouped = work.tile([P, SLOTS, P, PACK], BF16, align_bytes=64, name="grouped")
-        for pair in range(PAIRS):
-            regroup(turned[pair], pair, grouped)
+        regroup(turned[0], 0, grouped)
+        inverse = inverse_root(totals, 0, SLOTS)
+        regroup(turned[1], 1, grouped)
         w_codes = const.tile([P, D], U32, align_bytes=64)
         w_scales = const.tile([P, D], U8, align_bytes=64)
         w_grouped = const.tile([P, SLOTS, P, PACK], BF16, align_bytes=64)
         for pair in range(PAIRS):
-            regroup(turn(w_rows, pair), pair, w_grouped)
+            regroup(turn(w_rows, pair, product_banks, "product"), pair, w_grouped)
         bias = const.tile([P, D], F32)
-        bias_bank = turned_banks.tile([P, D], F32, name="turned")
+        bias_bank = product_banks.tile([P, D], F32, name="product")
         nc.tensor.matmul(bias_bank[:], lhsT=ones_row[:], rhs=bias_row[:], start=True, stop=True)
         nc.scalar.copy(out=bias[:], in_=bias_bank[:])
 
@@ -248,12 +261,18 @@ def tile_crossattention_pa_t_kernel(tc, features, fn_w, Wk_w, Wk_b, kn_w, out):
                 if i >= 1:
                     add_bias(products[s], biased[i - 1], s)
                     scalar_square_sum(biased[i - 1][:, s, :], totals[:, SLOTS + s : SLOTS + s + 1])
-                if s == (2 if i + 1 < GROUPS else 1):
+                if i == GROUPS - 1 and s == 1:
+                    for k in SCALAR_SLOTS[i - 2]:
+                        scalar_scale(i - 2, k, inverse[:, SLOTS + k : SLOTS + k + 1])
+                if s == 2:
                     quantise(grouped, codes, scales)
                     if i >= 2:
                         released = release(inverse)
+            if i == GROUPS - 2:
+                for s in SCALAR_SLOTS[i - 2]:
+                    scalar_scale(i - 2, s, inverse[:, SLOTS + s : SLOTS + s + 1])
             if i == 0:
-                for s in (2, 3):
+                for s in range(2, SLOTS):
                     vector_square_sum(x_rows[2][:, s, :], totals[:, s : s + 1])
             if i >= 2:
                 finish(i - 2, biased[i - 2], finished[i - 2], inverse, released)
@@ -279,6 +298,7 @@ def tile_crossattention_pa_t_kernel(tc, features, fn_w, Wk_w, Wk_b, kn_w, out):
                 regroup(turned[0], 0, grouped)
             inverse = inverse_root(totals, 0 if i + 2 < GROUPS else SLOTS, 2 * SLOTS if i >= 1 else SLOTS)
 
+        g = GROUPS - 1
         last = sums.tile([P, SLOTS, D], F32, name="biased")
         totals = small.tile([P, 2 * SLOTS], F32, name="totals")
         inverses = []
@@ -287,8 +307,10 @@ def tile_crossattention_pa_t_kernel(tc, features, fn_w, Wk_w, Wk_b, kn_w, out):
                 add_bias(products[s], last, s)
                 scalar_square_sum(last[:, s, :], totals[:, s : s + 1])
             inverses.append(inverse_root(totals, 2 * pair, 2 * pair + 2))
-        finish(GROUPS - 2, biased[GROUPS - 2], finished[GROUPS - 2], inverse, inverse[:, SLOTS:])
-        for pair in range(PAIRS):
-            for s in (2 * pair, 2 * pair + 1):
-                vector_finish(last, last, s, 0, inverses[pair][:, s : s + 1])
-                nc.sync.dma_start(out=out_dram[GROUPS - 1, :, s, :], in_=last[:, s, :])
+        finish(g - 1, biased[g - 1], finished[g - 1], inverse, inverse[:, SLOTS:])
+        for s in SCALAR_SLOTS[g - 1]:
+            scalar_scale(g - 1, s, inverse[:, SLOTS + s : SLOTS + s + 1])
+            nc.scalar.dma_start(out=out_dram[g - 1, :, s, :], in_=finished[g - 1][:, s, :])
+        for s in range(SLOTS):
+            vector_finish(last, last, s, 0, inverses[s // 2][:, s : s + 1])
+            nc.sync.dma_start(out=out_dram[g, :, s, :], in_=last[:, s, :])

@@ -19,8 +19,10 @@ GROUPS = TOKENS // (P * SLOTS)
 EPS = 1e-6
 GPSIMD_COLUMNS = 2 * D + D // 2
 
-LAST_COLUMNS = {GROUPS - 3: 3 * D, GROUPS - 2: 2 * D}
-SCALAR_SLOTS = {GROUPS - 4: (1, 2), GROUPS - 3: (2,), GROUPS - 2: (0, 1)}
+LAST_COLUMNS = {GROUPS - 3: 3 * D, GROUPS - 2: 2 * D, GROUPS - 1: 0}
+SCALAR_SLOTS = {GROUPS - 4: (2,), GROUPS - 3: (2,), GROUPS - 2: ()}
+
+STORES = {GROUPS - 3: ((2, 4), (0, 2)), GROUPS - 2: ((2, 3), (3, 4))}
 
 FLOPS = 2 * TOKENS * D * D
 
@@ -195,11 +197,8 @@ def tile_crossattention_pa_t_kernel(tc, features, fn_w, Wk_w, Wk_b, kn_w, out):
                     )
                 if ours < D:
                     vector_finish(biased, finished, s, ours, inverse[:, SLOTS + s : SLOTS + s + 1])
-            if g < GROUPS - 2:
-                nc.sync.dma_start(out=out_dram[g], in_=finished[:])
-            else:
-                first = len(SCALAR_SLOTS[g])
-                nc.sync.dma_start(out=out_dram[g, :, first:, :], in_=finished[:, first:, :])
+            for first, last in STORES.get(g, ((0, SLOTS),)):
+                nc.sync.dma_start(out=out_dram[g, :, first:last, :], in_=finished[:, first:last, :])
 
         gains = gain_bank.tile([P, 2, D], BF16)
         nc.tensor.matmul(gains[:, 0, :], lhsT=ones_row[:], rhs=fn_row[:], start=True, stop=True)
@@ -247,8 +246,7 @@ def tile_crossattention_pa_t_kernel(tc, features, fn_w, Wk_w, Wk_b, kn_w, out):
             totals = small.tile([P, 2 * SLOTS], F32, name="totals")
             if i == 0:
                 next_grouped = work.tile([P, SLOTS, P, PACK], BF16, align_bytes=64, name="grouped")
-                for pair in range(PAIRS):
-                    regroup(turned[pair], pair, next_grouped)
+                regroup(turned[0], 0, next_grouped)
             codes = work.tile([P, SLOTS * P], U32, align_bytes=64)
             scales = work.tile([P, SLOTS * P], U8, align_bytes=64)
             if i >= 1:
@@ -256,6 +254,10 @@ def tile_crossattention_pa_t_kernel(tc, features, fn_w, Wk_w, Wk_b, kn_w, out):
             for s in range(SLOTS):
                 if i + 2 < GROUPS and not (i == 0 and s >= 2):
                     scalar_square_sum(x_rows[i + 2][:, s, :], totals[:, s : s + 1])
+                if i == 0 and s == 0:
+                    regroup(turned[1], 1, next_grouped)
+                if i == 1 and s == 0:
+                    inverse = inverse_root(first_totals, 0, SLOTS)
                 if i >= 2 and s == 0:
                     regroup(turned[1], 1, grouped)
                 if i >= 1:
@@ -296,20 +298,26 @@ def tile_crossattention_pa_t_kernel(tc, features, fn_w, Wk_w, Wk_b, kn_w, out):
                     turned[pair] = turn(normed, pair)
                 grouped = work.tile([P, SLOTS, P, PACK], BF16, align_bytes=64, name="grouped")
                 regroup(turned[0], 0, grouped)
-            inverse = inverse_root(totals, 0 if i + 2 < GROUPS else SLOTS, 2 * SLOTS if i >= 1 else SLOTS)
+            if i == 0:
+                first_totals = totals
+            else:
+                inverse = inverse_root(totals, 0 if i + 2 < GROUPS else SLOTS, 2 * SLOTS)
 
         g = GROUPS - 1
         last = sums.tile([P, SLOTS, D], F32, name="biased")
         totals = small.tile([P, 2 * SLOTS], F32, name="totals")
         inverses = []
-        for pair in range(PAIRS):
-            for s in (2 * pair, 2 * pair + 1):
+        early = 4
+        for s in range(SLOTS):
+            if s < early:
                 add_bias(products[s], last, s)
                 scalar_square_sum(last[:, s, :], totals[:, s : s + 1])
-            inverses.append(inverse_root(totals, 2 * pair, 2 * pair + 2))
+            if s % 2 and s < early:
+                inverses.append(inverse_root(totals, s - 1, s + 1))
         finish(g - 1, biased[g - 1], finished[g - 1], inverse, inverse[:, SLOTS:])
         for s in SCALAR_SLOTS[g - 1]:
             scalar_scale(g - 1, s, inverse[:, SLOTS + s : SLOTS + s + 1])
+        for s in (0, 1):
             nc.scalar.dma_start(out=out_dram[g - 1, :, s, :], in_=finished[g - 1][:, s, :])
         for s in range(SLOTS):
             vector_finish(last, last, s, 0, inverses[s // 2][:, s : s + 1])

@@ -64,11 +64,11 @@ def tile_crossattention_pa_t_kernel(tc, features, fn_w, Wk_w, Wk_b, kn_w, out):
         for g in range(GROUPS):
             x_g = resident.tile([P, SLOTS, D], BF16, name="x%d" % g)
             x_rows.append(x_g)
-            if g == 0:
+            if g <= 1:
                 for pair in range(PAIRS):
                     slots = slice(2 * pair, 2 * pair + 2)
                     nc.sync.dma_start(out=x_g[:, slots, :], in_=x_dram[g, :, slots, :])
-                    if pair == 0:
+                    if g == 0 and pair == 0:
                         load_row(fn_row[0:1, :], fn_w)
             else:
                 nc.sync.dma_start(out=x_g[:], in_=x_dram[g])
@@ -210,25 +210,25 @@ def tile_crossattention_pa_t_kernel(tc, features, fn_w, Wk_w, Wk_b, kn_w, out):
             scalar_square_sum(x_rows[0][:, 2 * pair, :], totals[:, 2 * pair : 2 * pair + 1])
             vector_square_sum(x_rows[0][:, 2 * pair + 1, :], totals[:, 2 * pair + 1 : 2 * pair + 2])
             inverses.append(inverse_root(totals, 2 * pair, 2 * pair + 2))
+        totals = small.tile([P, 2 * SLOTS], F32, name="totals")
+        for s in range(SLOTS - 1):
+            scalar_square_sum(x_rows[1][:, s, :], totals[:, s : s + 1])
+        w_turned = {}
         for pair in range(PAIRS):
             for s in (2 * pair, 2 * pair + 1):
                 normalise(0, s, inverses[pair], normed)
+            if pair == 0:
+                vector_square_sum(x_rows[1][:, SLOTS - 1, :], totals[:, SLOTS - 1 : SLOTS])
             turned[pair] = turn(normed, pair)
-
-        totals = small.tile([P, 2 * SLOTS], F32, name="totals")
-        for s in range(3):
-            scalar_square_sum(x_rows[1][:, s, :], totals[:, s : s + 1])
-        for s in range(3, SLOTS):
-            vector_square_sum(x_rows[1][:, s, :], totals[:, s : s + 1])
-        grouped = work.tile([P, SLOTS, P, PACK], BF16, align_bytes=64, name="grouped")
-        regroup(turned[0], 0, grouped)
+            w_turned[pair] = turn(w_rows, pair, product_banks, "product")
         inverse = inverse_root(totals, 0, SLOTS)
-        regroup(turned[1], 1, grouped)
+        grouped = work.tile([P, SLOTS, P, PACK], BF16, align_bytes=64, name="grouped")
         w_codes = const.tile([P, D], U32, align_bytes=64)
         w_scales = const.tile([P, D], U8, align_bytes=64)
         w_grouped = const.tile([P, SLOTS, P, PACK], BF16, align_bytes=64)
         for pair in range(PAIRS):
-            regroup(turn(w_rows, pair, product_banks, "product"), pair, w_grouped)
+            regroup(turned[pair], pair, grouped)
+            regroup(w_turned[pair], pair, w_grouped)
         bias = const.tile([P, D], F32)
         bias_bank = product_banks.tile([P, D], F32, name="product")
         nc.tensor.matmul(bias_bank[:], lhsT=ones_row[:], rhs=bias_row[:], start=True, stop=True)
@@ -256,8 +256,10 @@ def tile_crossattention_pa_t_kernel(tc, features, fn_w, Wk_w, Wk_b, kn_w, out):
                     scalar_square_sum(x_rows[i + 2][:, s, :], totals[:, s : s + 1])
                 if i == 0 and s == 0:
                     regroup(turned[1], 1, next_grouped)
-                if i == 1 and s == 0:
-                    inverse = inverse_root(first_totals, 0, SLOTS)
+                if i >= 1 and s == 0:
+                    if i >= 2:
+                        regroup(turned[0], 0, grouped)
+                    inverse = inverse_root(*pending)
                 if i >= 2 and s == 0:
                     regroup(turned[1], 1, grouped)
                 if i >= 1:
@@ -297,11 +299,9 @@ def tile_crossattention_pa_t_kernel(tc, features, fn_w, Wk_w, Wk_b, kn_w, out):
                         normalise(i + 1, s, inverse, normed)
                     turned[pair] = turn(normed, pair)
                 grouped = work.tile([P, SLOTS, P, PACK], BF16, align_bytes=64, name="grouped")
-                regroup(turned[0], 0, grouped)
-            if i == 0:
-                first_totals = totals
-            else:
-                inverse = inverse_root(totals, 0 if i + 2 < GROUPS else SLOTS, 2 * SLOTS)
+            pending = (totals, 0 if i + 2 < GROUPS else SLOTS, 2 * SLOTS if i >= 1 else SLOTS)
+            if i == GROUPS - 1:
+                inverse = inverse_root(*pending)
 
         g = GROUPS - 1
         last = sums.tile([P, SLOTS, D], F32, name="biased")

@@ -34,7 +34,7 @@ def tile_crossattention_pa_t_kernel(tc, features, fn_w, Wk_w, Wk_b, kn_w, out):
 
     with tc.tile_pool(name="const", bufs=1) as const, tc.tile_pool(name="resident", bufs=1) as resident, tc.tile_pool(
         name="work", bufs=2
-    ) as work, tc.tile_pool(name="sums", bufs=3) as sums, tc.tile_pool(name="result", bufs=5) as result, tc.tile_pool(name="small", bufs=4) as small, tc.psum_pool(
+    ) as work, tc.tile_pool(name="sums", bufs=3) as sums, tc.tile_pool(name="result", bufs=5) as result, tc.tile_pool(name="small", bufs=8) as small, tc.tile_pool(name="unread", bufs=16) as unread, tc.psum_pool(
         name="turned_banks", bufs=3
     ) as turned_banks, tc.psum_pool(name="product_banks", bufs=4) as product_banks, tc.psum_pool(
         name="gain_bank", bufs=1
@@ -80,11 +80,11 @@ def tile_crossattention_pa_t_kernel(tc, features, fn_w, Wk_w, Wk_b, kn_w, out):
                 nc.sync.dma_start(out=kn_gain_sbuf[:, 0, :], in_=kn_w.partition_broadcast(P))
 
         def scalar_square_sum(row, total):
-            squares = small.tile([P, D], BF16)
+            squares = unread.tile([P, D], BF16, name="unread")
             nc.scalar.activation(out=squares[:], in_=row, func=ACT.Square, accum_out=total)
 
         def vector_square_sum(row, total):
-            products = small.tile([P, D], BF16)
+            products = unread.tile([P, D], BF16, name="unread")
             nc.vector.scalar_tensor_tensor(
                 out=products[:], in0=row, scalar=1.0, in1=row, op0=ALU.mult, op1=ALU.mult, accum_out=total
             )
@@ -256,22 +256,20 @@ def tile_crossattention_pa_t_kernel(tc, features, fn_w, Wk_w, Wk_b, kn_w, out):
                     scalar_square_sum(x_rows[i + 2][:, s, :], totals[:, s : s + 1])
                 if i == 0 and s == 0:
                     regroup(turned[1], 1, next_grouped)
-                if i >= 1 and s == 0:
-                    if i >= 2:
-                        regroup(turned[0], 0, grouped)
-                    inverse = inverse_root(*pending)
                 if i >= 2 and s == 0:
+                    regroup(turned[0], 0, grouped)
                     regroup(turned[1], 1, grouped)
                 if i >= 1:
                     add_bias(products[s], biased[i - 1], s)
+                if i >= 1:
                     scalar_square_sum(biased[i - 1][:, s, :], totals[:, SLOTS + s : SLOTS + s + 1])
+                if i >= 1 and s == 0:
+                    inverse = inverse_root(*pending)
                 if i == GROUPS - 1 and s == 1:
                     for k in SCALAR_SLOTS[i - 2]:
                         scalar_scale(i - 2, k, inverse[:, SLOTS + k : SLOTS + k + 1])
                 if s == 2:
                     quantise(grouped, codes, scales)
-                    if i >= 2:
-                        released = release(inverse)
             if i == GROUPS - 2:
                 for s in SCALAR_SLOTS[i - 2]:
                     scalar_scale(i - 2, s, inverse[:, SLOTS + s : SLOTS + s + 1])
@@ -279,7 +277,7 @@ def tile_crossattention_pa_t_kernel(tc, features, fn_w, Wk_w, Wk_b, kn_w, out):
                 for s in range(2, SLOTS):
                     vector_square_sum(x_rows[2][:, s, :], totals[:, s : s + 1])
             if i >= 2:
-                finish(i - 2, biased[i - 2], finished[i - 2], inverse, released)
+                finish(i - 2, biased[i - 2], finished[i - 2], inverse, inverse[:, SLOTS:])
             if i >= 1:
                 finished[i - 1] = gain_shared(i - 1, biased[i - 1])
             for s in range(SLOTS):

@@ -17,7 +17,7 @@ SLOTS = 4
 PAIRS = SLOTS // 2
 GROUPS = TOKENS // (P * SLOTS)
 EPS = 1e-6
-GPSIMD_COLUMNS = 2 * D + D // 2
+GPSIMD_COLUMNS = 2 * D + 9 * D // 16
 
 LAST_COLUMNS = {GROUPS - 3: 3 * D, GROUPS - 2: 2 * D, GROUPS - 1: 0}
 SCALAR_SLOTS = {GROUPS - 4: (2,), GROUPS - 3: (2,), GROUPS - 2: ()}

import concourse.mybir as mybir
from concourse.masks import make_identity

BF16 = mybir.dt.bfloat16
F32 = mybir.dt.float32
U32 = mybir.dt.uint32
U8 = mybir.dt.uint8
FP8X4 = mybir.dt.float8_e4m3fn_x4
ACT = mybir.ActivationFunctionType
ALU = mybir.AluOpType

P = 128
PACK = 4
D = 512
TOKENS = 8 * 1024
SLOTS = 4
PAIRS = SLOTS // 2
GROUPS = TOKENS // (P * SLOTS)
EPS = 1e-6
GPSIMD_COLUMNS = 2 * D + 9 * D // 16

LAST_COLUMNS = {GROUPS - 3: 3 * D, GROUPS - 2: 2 * D, GROUPS - 1: 0}
SCALAR_SLOTS = {GROUPS - 4: (2,), GROUPS - 3: (2,), GROUPS - 2: ()}

STORES = {GROUPS - 3: ((2, 4), (0, 2)), GROUPS - 2: ((2, 3), (3, 4))}

FLOPS = 2 * TOKENS * D * D


def tile_crossattention_pa_t_kernel(tc, features, fn_w, Wk_w, Wk_b, kn_w, out):
    nc = tc.nc
    x_dram = features.flatten_outer_dims().rearrange("(g p s) k -> g p s k", p=P, s=SLOTS)
    out_dram = out.flatten_outer_dims().rearrange("(g p s) o -> g p s o", p=P, s=SLOTS)

    with tc.tile_pool(name="const", bufs=1) as const, tc.tile_pool(name="resident", bufs=1) as resident, tc.tile_pool(
        name="work", bufs=2
    ) as work, tc.tile_pool(name="sums", bufs=3) as sums, tc.tile_pool(name="result", bufs=5) as result, tc.tile_pool(name="small", bufs=8) as small, tc.tile_pool(name="unread", bufs=16) as unread, tc.psum_pool(
        name="turned_banks", bufs=3
    ) as turned_banks, tc.psum_pool(name="product_banks", bufs=4) as product_banks, tc.psum_pool(
        name="gain_bank", bufs=1
    ) as gain_bank, tc.manual_schedule():
        eps = const.tile([P, 1], F32)
        nc.vector.memset(eps[:], EPS)
        warm = const.tile([P, 1], F32)
        nc.scalar.activation(out=warm[:], in_=eps[:], func=ACT.Abs_reciprocal_sqrt)
        ident = const.tile([P, P], F32)
        make_identity(nc, ident[:])
        fn_row = const.tile([P, D], BF16)
        nc.vector.memset(fn_row[:], 0.0)
        kn_row = const.tile([P, D], BF16)
        nc.gpsimd.memset(kn_row[:], 0.0)
        bias_row = const.tile([P, D], BF16)
        nc.gpsimd.memset(bias_row[:], 0.0)
        ones_row = const.tile([P, P], BF16)
        nc.vector.memset(ones_row[:], 0.0)
        nc.vector.memset(ones_row[0:1, :], 1.0)

        def load_row(row, source):
            nc.sync.dma_start(out=row, in_=source.rearrange("(a d) -> a d", a=1))

        kn_gain_sbuf = const.tile([P, SLOTS, D], BF16)
        x_rows = []
        w_rows = const.tile([P, SLOTS, D], BF16)
        for g in range(GROUPS):
            x_g = resident.tile([P, SLOTS, D], BF16, name="x%d" % g)
            x_rows.append(x_g)
            if g <= 1:
                for pair in range(PAIRS):
                    slots = slice(2 * pair, 2 * pair + 2)
                    nc.sync.dma_start(out=x_g[:, slots, :], in_=x_dram[g, :, slots, :])
                    if g == 0 and pair == 0:
                        load_row(fn_row[0:1, :], fn_w)
            else:
                nc.sync.dma_start(out=x_g[:], in_=x_dram[g])
            if g == 1:
                nc.sync.dma_start(out=w_rows[:], in_=Wk_w.rearrange("(s p) k -> p s k", p=P))
                load_row(kn_row[0:1, :], kn_w)
                load_row(bias_row[0:1, :], Wk_b)
            if g == 5:
                nc.sync.dma_start(out=kn_gain_sbuf[:, 0, :], in_=kn_w.partition_broadcast(P))

        def scalar_square_sum(row, total):
            squares = unread.tile([P, D], BF16, name="unread")
            nc.scalar.activation(out=squares[:], in_=row, func=ACT.Square, accum_out=total)

        def vector_square_sum(row, total):
            products = unread.tile([P, D], BF16, name="unread")
            nc.vector.scalar_tensor_tensor(
                out=products[:], in0=row, scalar=1.0, in1=row, op0=ALU.mult, op1=ALU.mult, accum_out=total
            )

        def inverse_root(totals, first, last):
            inverse = small.tile([P, 2 * SLOTS], F32)
            nc.scalar.activation(
                out=inverse[:, first:last],
                in_=totals[:, first:last],
                func=ACT.Abs_reciprocal_sqrt,
                scale=1.0 / D,
                bias=eps[:],
            )
            return inverse

        def release(inverse):
            released = small.tile([P, SLOTS], F32)
            nc.vector.tensor_copy(out=released[:], in_=inverse[:, SLOTS:])
            return released

        def normalise(g, s, inverse, normed):
            nc.vector.scalar_tensor_tensor(
                out=normed[:, s, :],
                in0=x_rows[g][:, s, :],
                scalar=inverse[:, s : s + 1],
                in1=gains[:, 0, :],
                op0=ALU.mult,
                op1=ALU.mult,
            )

        def turn(rows, pair, pool=turned_banks, name="turned"):
            turned = pool.tile([P, 2, 2, P], F32, name=name)
            for s in range(2):
                words = rows[:, 2 * pair + s, :].bitcast(F32)
                for u in range(2):
                    nc.tensor.transpose(turned[:, s, u, :], words[:, u : D // 2 : 2], ident[:])
            return turned

        def regroup(turned, pair, grouped, copy=nc.scalar.copy):
            copy(
                out=grouped[:, 2 * pair : 2 * pair + 2, :, :].rearrange("p s r t -> p (s r t)").bitcast(F32),
                in_=turned[:].rearrange("p s u r -> p s r u"),
            )

        def quantise(grouped, codes, scales):
            nc.vector.quantize_mx(
                out=codes[:].bitcast(FP8X4), scales=scales[:], in_=grouped[:].rearrange("p s r t -> p (s r t)")
            )

        def multiply(codes, scales, s):
            product = product_banks.tile([P, D], F32, name="product")
            nc.tensor.matmul_mx(
                out=product[:],
                lhsT=codes[:, s * P : (s + 1) * P].bitcast(FP8X4),
                lhsT_scale=scales[:, s * P : (s + 1) * P],
                rhs=w_codes[:].bitcast(FP8X4),
                rhs_scale=w_scales[:],
                start=True,
                stop=True,
            )
            return product

        def add_bias(product, biased, s):
            nc.vector.tensor_tensor(out=biased[:, s, :], in0=product[:], in1=bias[:], op=ALU.add)

        def vector_finish(biased, finished, s, first, inverse):
            nc.vector.scalar_tensor_tensor(
                out=finished[:, s, first:],
                in0=biased[:, s, first:],
                scalar=inverse,
                in1=gains[:, 1, first:],
                op0=ALU.mult,
                op1=ALU.mult,
            )

        def gpsimd_columns(g):
            return LAST_COLUMNS.get(g, GPSIMD_COLUMNS)

        def slot_columns(g, s):
            return min(max(gpsimd_columns(g) - s * D, 0), D)

        def scalar_scale(g, s, inverse):
            ours = slot_columns(g, s)
            nc.scalar.activation(
                out=finished[g][:, s, :ours], in_=finished[g][:, s, :ours], func=ACT.Copy, scale=inverse
            )

        def gain_shared(g, biased):
            finished = result.tile([P, SLOTS, D], F32, name="finished")
            shared = gpsimd_columns(g)
            nc.gpsimd.tensor_tensor(
                out=finished[:].rearrange("p s o -> p (s o)")[:, :shared],
                in0=biased[:].rearrange("p s o -> p (s o)")[:, :shared],
                in1=kn_gain_sbuf[:].rearrange("p s o -> p (s o)")[:, :shared],
                op=ALU.mult,
            )
            return finished

        def finish(g, biased, finished, inverse, released):
            for s in range(SLOTS):
                ours = slot_columns(g, s)
                if ours > 0 and s not in SCALAR_SLOTS.get(g, ()):
                    nc.gpsimd.tensor_scalar(
                        out=finished[:, s, :ours],
                        in0=finished[:, s, :ours],
                        scalar1=released[:, s : s + 1],
                        scalar2=0.0,
                        op0=ALU.mult,
                        op1=ALU.add,
                    )
                if ours < D:
                    vector_finish(biased, finished, s, ours, inverse[:, SLOTS + s : SLOTS + s + 1])
            for first, last in STORES.get(g, ((0, SLOTS),)):
                nc.sync.dma_start(out=out_dram[g, :, first:last, :], in_=finished[:, first:last, :])

        gains = gain_bank.tile([P, 2, D], BF16)
        nc.tensor.matmul(gains[:, 0, :], lhsT=ones_row[:], rhs=fn_row[:], start=True, stop=True)
        totals = small.tile([P, 2 * SLOTS], F32, name="totals")
        normed = work.tile([P, SLOTS, D], BF16, name="normed")
        turned = {}
        inverses = []
        for pair in range(PAIRS):
            scalar_square_sum(x_rows[0][:, 2 * pair, :], totals[:, 2 * pair : 2 * pair + 1])
            vector_square_sum(x_rows[0][:, 2 * pair + 1, :], totals[:, 2 * pair + 1 : 2 * pair + 2])
            inverses.append(inverse_root(totals, 2 * pair, 2 * pair + 2))
        totals = small.tile([P, 2 * SLOTS], F32, name="totals")
        for s in range(SLOTS - 1):
            scalar_square_sum(x_rows[1][:, s, :], totals[:, s : s + 1])
        w_turned = {}
        for pair in range(PAIRS):
            for s in (2 * pair, 2 * pair + 1):
                normalise(0, s, inverses[pair], normed)
            if pair == 0:
                vector_square_sum(x_rows[1][:, SLOTS - 1, :], totals[:, SLOTS - 1 : SLOTS])
            turned[pair] = turn(normed, pair)
            w_turned[pair] = turn(w_rows, pair, product_banks, "product")
        inverse = inverse_root(totals, 0, SLOTS)
        grouped = work.tile([P, SLOTS, P, PACK], BF16, align_bytes=64, name="grouped")
        w_codes = const.tile([P, D], U32, align_bytes=64)
        w_scales = const.tile([P, D], U8, align_bytes=64)
        w_grouped = const.tile([P, SLOTS, P, PACK], BF16, align_bytes=64)
        for pair in range(PAIRS):
            regroup(turned[pair], pair, grouped)
            regroup(w_turned[pair], pair, w_grouped)
        bias = const.tile([P, D], F32)
        bias_bank = product_banks.tile([P, D], F32, name="product")
        nc.tensor.matmul(bias_bank[:], lhsT=ones_row[:], rhs=bias_row[:], start=True, stop=True)
        nc.scalar.copy(out=bias[:], in_=bias_bank[:])

        normed = work.tile([P, SLOTS, D], BF16, name="normed")
        for pair in range(PAIRS):
            for s in (2 * pair, 2 * pair + 1):
                normalise(1, s, inverse, normed)
            turned[pair] = turn(normed, pair)
        quantise(w_grouped, w_codes, w_scales)

        products, biased, finished = {}, {}, {}
        for i in range(GROUPS):
            totals = small.tile([P, 2 * SLOTS], F32, name="totals")
            if i == 0:
                next_grouped = work.tile([P, SLOTS, P, PACK], BF16, align_bytes=64, name="grouped")
                regroup(turned[0], 0, next_grouped)
            codes = work.tile([P, SLOTS * P], U32, align_bytes=64)
            scales = work.tile([P, SLOTS * P], U8, align_bytes=64)
            if i >= 1:
                biased[i - 1] = sums.tile([P, SLOTS, D], F32, name="biased")
            for s in range(SLOTS):
                if i + 2 < GROUPS and not (i == 0 and s >= 2):
                    scalar_square_sum(x_rows[i + 2][:, s, :], totals[:, s : s + 1])
                if i == 0 and s == 0:
                    regroup(turned[1], 1, next_grouped)
                if i >= 2 and s == 0:
                    regroup(turned[0], 0, grouped)
                    regroup(turned[1], 1, grouped)
                if i >= 1:
                    add_bias(products[s], biased[i - 1], s)
                if i >= 1:
                    scalar_square_sum(biased[i - 1][:, s, :], totals[:, SLOTS + s : SLOTS + s + 1])
                if i >= 1 and s == 0:
                    inverse = inverse_root(*pending)
                if i == GROUPS - 1 and s == 1:
                    for k in SCALAR_SLOTS[i - 2]:
                        scalar_scale(i - 2, k, inverse[:, SLOTS + k : SLOTS + k + 1])
                if s == 2:
                    quantise(grouped, codes, scales)
            if i == GROUPS - 2:
                for s in SCALAR_SLOTS[i - 2]:
                    scalar_scale(i - 2, s, inverse[:, SLOTS + s : SLOTS + s + 1])
            if i == 0:
                for s in range(2, SLOTS):
                    vector_square_sum(x_rows[2][:, s, :], totals[:, s : s + 1])
            if i >= 2:
                finish(i - 2, biased[i - 2], finished[i - 2], inverse, inverse[:, SLOTS:])
            if i >= 1:
                finished[i - 1] = gain_shared(i - 1, biased[i - 1])
            for s in range(SLOTS):
                products[s] = multiply(codes, scales, s)
            if i == 0:
                nc.tensor.matmul(gains[:, 1, :], lhsT=ones_row[:], rhs=kn_row[:], start=True, stop=True)
                for s in range(1, -(-GPSIMD_COLUMNS // D)):
                    nc.gpsimd.tensor_scalar(
                        out=kn_gain_sbuf[:, s, :], in0=kn_gain_sbuf[:, 0, :], scalar1=1.0, scalar2=0.0, op0=ALU.mult, op1=ALU.add
                    )
            if i == 0:
                grouped = next_grouped
            elif i + 1 < GROUPS:
                normed = work.tile([P, SLOTS, D], BF16, name="normed")
                for pair in range(PAIRS):
                    for s in (2 * pair, 2 * pair + 1):
                        normalise(i + 1, s, inverse, normed)
                    turned[pair] = turn(normed, pair)
                grouped = work.tile([P, SLOTS, P, PACK], BF16, align_bytes=64, name="grouped")
            pending = (totals, 0 if i + 2 < GROUPS else SLOTS, 2 * SLOTS if i >= 1 else SLOTS)
            if i == GROUPS - 1:
                inverse = inverse_root(*pending)

        g = GROUPS - 1
        last = sums.tile([P, SLOTS, D], F32, name="biased")
        totals = small.tile([P, 2 * SLOTS], F32, name="totals")
        inverses = []
        early = 4
        for s in range(SLOTS):
            if s < early:
                add_bias(products[s], last, s)
                scalar_square_sum(last[:, s, :], totals[:, s : s + 1])
            if s % 2 and s < early:
                inverses.append(inverse_root(totals, s - 1, s + 1))
        finish(g - 1, biased[g - 1], finished[g - 1], inverse, inverse[:, SLOTS:])
        for s in SCALAR_SLOTS[g - 1]:
            scalar_scale(g - 1, s, inverse[:, SLOTS + s : SLOTS + s + 1])
        for s in (0, 1):
            nc.scalar.dma_start(out=out_dram[g - 1, :, s, :], in_=finished[g - 1][:, s, :])
        for s in range(SLOTS):
            vector_finish(last, last, s, 0, inverses[s // 2][:, s : s + 1])
            nc.sync.dma_start(out=out_dram[g, :, s, :], in_=last[:, s, :])
